import numpy as np
import ml_dtypes


def mxq(x, axis, fmt="e4m3"):
    dtype, down = {"e4m3": (ml_dtypes.float8_e4m3fn, 7), "e5m2": (ml_dtypes.float8_e5m2, 14)}[fmt]
    v = np.moveaxis(np.asarray(x, np.float32).astype(ml_dtypes.bfloat16).astype(np.float64), axis, -1)
    blocks = v.reshape(v.shape[:-1] + (-1, 32))
    amax = np.abs(blocks).max(-1, keepdims=True)
    byte = np.maximum(np.where(amax > 0, np.frexp(amax)[1] - 1 + 127, 0) - down, 1)
    scale = np.exp2(byte - 127.0)
    codes = (blocks / scale).astype(np.float32).astype(dtype).astype(np.float64)
    return np.moveaxis((codes * scale).reshape(v.shape), -1, axis)


WIDE = False


def mx_kscale(k):
    if not WIDE:
        return np.ones(k)
    levels = np.array([10, -10, 5, -5, 0])
    a = np.random.permutation(np.resize(levels, k // 512 * 4)).reshape(k // 512, 4)
    idx = np.arange(k)
    return np.exp2(a[idx // 512, idx % 128 // 32])


BF16 = ml_dtypes.bfloat16


def bf(x):
    return np.asarray(x, np.float32).astype(BF16)


def f64(x):
    return np.asarray(x).astype(np.float64)


B, S, D, H, KD, VD = 32, 32, 1024, 8, 128, 128
E = H * VD
EPS = 1e-5


def silu(v):
    return v / (1.0 + np.exp(-v))


def setup_inputs():
    s = mx_kscale(D)
    amp = 10.0 ** np.random.uniform(-2.5, 0.5, (B, S, H, 1))
    ret = amp * (np.random.standard_normal((B, S, H, VD)) + 0.3 * np.random.standard_normal((B, S, H, 1)))
    return {"x": bf(np.random.standard_normal((B, S, D)) * s),
            "ret_cat": bf(ret.reshape(B, S, E)),
            "Wg": bf(np.random.standard_normal((D, E)) / np.sqrt(D) / s[:, None]),
            "bg": bf(np.random.standard_normal(E) * 0.2),
            "Wo": bf(np.random.standard_normal((E, D)) / np.sqrt(E)),
            "bo": bf(np.random.standard_normal(D) * 0.2)}


def reference(x, ret_cat, Wg, bg, Wo, bo):
    gate = silu((mxq(f64(x), 2, "e4m3") @ mxq(f64(Wg), 0, "e4m3")) + f64(bg))
    g = f64(ret_cat).reshape(B * S, H, VD)
    mu = g.mean(-1, keepdims=True)
    var = g.var(-1, keepdims=True)
    cat = ((g - mu) / np.sqrt(var + EPS)).reshape(B, S, E)
    h = gate * cat
    return (mxq(h, 2, "e4m3") @ mxq(f64(Wo), 0, "e4m3")) + f64(bo)

@@ -1,0 +1,482 @@
+from contextlib import ExitStack
+
+import concourse.mybir as mybir
+from concourse.masks import make_identity
+
+FLOPS = 2 * 2 * 1024 * 1024 * 1024
+
+BF16 = mybir.dt.bfloat16
+F32 = mybir.dt.float32
+U32 = mybir.dt.uint32
+U8 = mybir.dt.uint8
+FP8X4 = mybir.dt.float8_e4m3fn_x4
+ACT = mybir.ActivationFunctionType
+ALU = mybir.AluOpType
+AX = mybir.AxisListType
+
+P = 128
+EPS = 1e-5
+PIN = True
+GRPBUFS = 4
+OUTBUFS = 4
+TPB = 3
+S1B = 3
+S2B = 2
+
+
+def tile_gatedmultiscaleretentionlayer_pa_kernel(tc, x, ret_cat, Wg, bg, Wo, bo, out):
+    nc = tc.nc
+    xv = x.flatten_outer_dims().rearrange("(p i) k -> p i k", i=8)
+    rv = ret_cat.flatten_outer_dims().rearrange("(p i) c -> p i c", i=8)
+    ov = out.flatten_outer_dims().rearrange("(p i) d -> p i d", i=8)
+
+    with ExitStack() as ctx:
+        const = ctx.enter_context(tc.tile_pool(name="const", bufs=1))
+        raw = ctx.enter_context(tc.tile_pool(name="raw", bufs=1))
+        grp = ctx.enter_context(tc.tile_pool(name="grp", bufs=GRPBUFS))
+        mxp = ctx.enter_context(tc.tile_pool(name="mxp", bufs=1))
+        stat = ctx.enter_context(tc.tile_pool(name="stat", bufs=1))
+        catp = ctx.enter_context(tc.tile_pool(name="catp", bufs=8))
+        gatep = ctx.enter_context(tc.tile_pool(name="gatep", bufs=1))
+        outp = ctx.enter_context(tc.tile_pool(name="outp", bufs=OUTBUFS))
+        psum = ctx.enter_context(tc.psum_pool(name="psum", bufs=1))
+        if PIN:
+            ctx.enter_context(tc.manual_schedule())
+
+        ident = const.tile([P, P], F32, name="ident")
+        bgpad = const.tile([P, P], BF16, name="bgpad")
+        bopad = const.tile([P, 1024], BF16, name="bopad")
+        ones = const.tile([P, P], BF16, name="ones")
+        epst = const.tile([P, 1], F32, name="epst")
+        warm = const.tile([P, 1], F32, name="warm")
+        bgf = const.tile([P, P], F32, name="bgf")
+        bgT = const.tile([P, 8], F32, name="bgT")
+        bo_bc = const.tile([P, 1024], F32, name="bo_bc")
+
+        def consts():
+            make_identity(nc, ident[:])
+            nc.vector.memset(bgpad[:], 0.0)
+            nc.vector.memset(bopad[:], 0.0)
+            nc.vector.memset(ones[:], 1.0)
+            nc.vector.memset(epst[:], 1.0)
+            nc.scalar.dma_start(out=bgpad[0:8, :], in_=bg.rearrange("(c p) -> c p", p=P))
+            nc.scalar.dma_start(out=bopad[0:1, :], in_=bo.rearrange("(o d) -> o d", o=1))
+            nc.scalar.activation(out=warm[:], in_=epst[:], func=ACT.Sqrt)
+
+        def bias():
+            nc.vector.tensor_copy(out=bgf[:], in_=bgpad[:])
+            pb = psum.tile([P, 512], F32, name="pb", tag="s2", bufs=S2B)
+            nc.tensor.transpose(pb[:, 0:P], bgf[:], ident[:])
+            nc.vector.tensor_copy(out=bgT[:], in_=pb[:, 0:8])
+            for h in range(2):
+                pbo = psum.tile([P, 512], F32, name="pbo", tag="s2", bufs=S2B)
+                nc.tensor.matmul(pbo[:], lhsT=ones[:], rhs=bopad[:, 512 * h : 512 * h + 512], start=True, stop=True)
+                nc.scalar.copy(out=bo_bc[:, 512 * h : 512 * h + 512], in_=pbo[:])
+
+        r_raw = [raw.tile([P, 1024], BF16, name="rraw%d" % i) for i in range(8)]
+        x_raw = [raw.tile([P, 2, 1024], BF16, name="xraw%d" % j) for j in range(4)]
+        w_raw = {(w, g): raw.tile([P, 4, 1024], BF16, name="%sraw%d" % (w, g)) for w in ("wg", "wo") for g in range(2)}
+
+        def ld_r(i):
+            nc.sync.dma_start(out=r_raw[i][:], in_=rv[:, i, :])
+
+        def ld_x(j):
+            nc.sync.dma_start(out=x_raw[j][:], in_=xv[:, 2 * j : 2 * j + 2, :])
+
+        def ld_wg(g):
+            nc.sync.dma_start(
+                out=w_raw[("wg", g)][:].rearrange("p (u e) n -> p u (e n)", u=2),
+                in_=Wg[512 * g : 512 * g + 512, :].rearrange("(u p e) n -> p u (e n)", u=2, e=2),
+            )
+
+        def ld_wo(g):
+            nc.sync.dma_start(
+                out=w_raw[("wo", g)][:], in_=Wo[512 * g : 512 * g + 512, :].rearrange("(t p) n -> p t n", p=P)
+            )
+
+        def mx_tiles(nm, width):
+            return (
+                mxp.tile([P, width], U32, name=nm + "q", align_bytes=64),
+                mxp.tile([P, width], U8, name=nm + "s", align_bytes=64),
+            )
+
+        xq = {(g, b): mx_tiles("x%d%d" % (g, b), 512) for g in range(2) for b in range(2)}
+        wq = {(w, g, h): mx_tiles("%s%d%d" % (w, g, h), 512) for w in ("wg", "wo") for g in range(2) for h in range(2)}
+        hq = {(g, b): mx_tiles("h%d%d" % (g, b), 512) for g in range(2) for b in range(2)}
+
+        def quantise(dst, src, lo=0, n=512):
+            nc.vector.quantize_mx(
+                out=dst[0][:, lo : lo + n].bitcast(FP8X4), scales=dst[1][:, lo : lo + n], in_=src[:, 4 * lo : 4 * lo + 4 * n]
+            )
+
+        rstd = stat.tile([P, 64], F32, name="rstd")
+        nmr = stat.tile([P, 64], F32, name="nmr")
+        st = [stat.tile([P, 16, 6], F32, name="st%d" % j) for j in range(4)]
+        sm = [stat.tile([P, 16, 2], F32, name="sm%d" % j) for j in range(4)]
+        sd = [stat.tile([P, 16], F32, name="sd%d" % j) for j in range(4)]
+
+        def bn(i):
+            for h in range(8):
+                nc.vector.bn_stats(out=st[i // 2][:, 8 * (i % 2) + h, :], in_=r_raw[i][:, P * h : P * h + P])
+
+        vv = {}
+
+        def cmb(j):
+            nc.vector.tensor_reduce(
+                out=sm[j][:], in_=st[j][:].rearrange("p n (a k) -> p n k a", a=2)[:, :, 1:3, :], axis=AX.X, op=ALU.add
+            )
+            d = stat.tile([P, 16], F32, name="d%d" % j)
+            nc.vector.tensor_tensor(out=d[:], in0=st[j][:, :, 1], in1=st[j][:, :, 4], op=ALU.subtract)
+            d2 = stat.tile([P, 16], F32, name="dd%d" % j)
+            nc.vector.tensor_tensor(out=d2[:], in0=d[:], in1=d[:], op=ALU.mult)
+            v = stat.tile([P, 16], F32, name="v%d" % j)
+            nc.vector.scalar_tensor_tensor(out=v[:], in0=d2[:], scalar=32.0, in1=sm[j][:, :, 1], op0=ALU.mult, op1=ALU.add)
+            ve = stat.tile([P, 16], F32, name="ve%d" % j)
+            nc.vector.tensor_scalar(out=ve[:], in0=v[:], scalar1=1.0 / 128.0, scalar2=EPS, op0=ALU.mult, op1=ALU.add)
+            vv[j] = ve
+
+        def sq(j):
+            nc.scalar.activation(out=sd[j][:], in_=vv[j][:], func=ACT.Sqrt)
+
+        def fin(j):
+            cols = slice(16 * j, 16 * j + 16)
+            nc.vector.reciprocal(out=rstd[:, cols], in_=sd[j][:])
+            nc.vector.scalar_tensor_tensor(
+                out=nmr[:, cols], in0=sm[j][:, :, 0], scalar=-0.5, in1=rstd[:, cols], op0=ALU.mult, op1=ALU.mult
+            )
+
+        catn = {}
+
+        def nrm(i):
+            t = catp.tile([P, 1024], F32, name="catn")
+            for h in range(8):
+                c = 8 * i + h
+                nc.scalar.activation(
+                    out=t[:, P * h : P * h + P],
+                    in_=r_raw[i][:, P * h : P * h + P],
+                    func=ACT.Identity,
+                    bias=nmr[:, c : c + 1],
+                    scale=rstd[:, c : c + 1],
+                )
+            catn[i] = t
+
+        xin = {}
+
+        xts = {}
+
+        def xTp(i):
+            xw = x_raw[i // 2][:, i % 2, :].bitcast(F32)
+            xt = psum.tile([P, 512], F32, name="xt", tag="s2", bufs=S2B)
+            for w in range(4):
+                nc.tensor.transpose(xt[:, P * w : P * w + P], xw[:, P * w : P * w + P], ident[:])
+            xts[i] = xt
+
+        def xTs(i):
+            b, ii = i // 4, i % 4
+            for g in range(2):
+                if (g, b) not in xin:
+                    xin[(g, b)] = grp.tile([P, 2048], BF16, name="xin", tag="xh", align_bytes=64)
+                nc.scalar.copy(
+                    out=xin[(g, b)][:].bitcast(F32)[:, 256 * ii : 256 * ii + 256].rearrange("p (r u) -> p r u", u=2),
+                    in_=xts[i][:, 256 * g : 256 * g + 256].rearrange("p (u r) -> p r u", u=2),
+                )
+
+        def xQ(g, b):
+            quantise(xq[(g, b)], xin[(g, b)])
+
+        win = {}
+
+        def rg(eng, w, g, h):
+            t = grp.tile([P, 2048], BF16, name="win", tag="win%d%d" % (g, h), bufs=1, align_bytes=64)
+            dst = t[:].rearrange("p (c i t) -> p c t i", i=4, t=4)
+            s = w_raw[(w, g)][:, :, 512 * h : 512 * h + 512].rearrange("p t (c i) -> p c t i", i=4)
+            if eng == "V":
+                nc.vector.tensor_copy(out=dst, in_=s)
+            elif eng == "S":
+                nc.scalar.copy(out=dst, in_=s)
+            else:
+                nc.gpsimd.tensor_scalar(out=dst, in0=s, scalar1=1.0, scalar2=0.0, op0=ALU.mult, op1=ALU.add)
+            win[(w, g, h)] = t
+
+        def wQ(w, g, h):
+            quantise(wq[(w, g, h)], win[(w, g, h)])
+
+        gate = {}
+
+        ps1 = {}
+
+        def s1p(b, c):
+            gr, t = c // 4, c % 4
+            ps = psum.tile([P, 512], F32, name="ps1", tag="s1", bufs=S1B)
+            for g in range(2):
+                cq, cs = wq[("wg", g, gr)]
+                nc.tensor.matmul_mx(
+                    out=ps[:],
+                    lhsT=cq[:, P * t : P * t + P].bitcast(FP8X4),
+                    lhsT_scale=cs[:, P * t : P * t + P],
+                    rhs=xq[(g, b)][0][:].bitcast(FP8X4),
+                    rhs_scale=xq[(g, b)][1][:],
+                    start=(g == 0),
+                    stop=(g == 1),
+                )
+            ps1[(b, c)] = ps
+
+        def s1a(b, c):
+            gr, t = c // 4, c % 4
+            if (b, gr) not in gate:
+                gate[(b, gr)] = gatep.tile([P, 4, 512], F32, name="gate%d%d" % (b, gr))
+            nc.scalar.activation(
+                out=gate[(b, gr)][:, t, :], in_=ps1[(b, c)][:], func=ACT.Silu, bias=bgT[:, c : c + 1], scale=1.0
+            )
+
+        hin = {}
+        cts = {}
+
+        def ct(i, gr):
+            t_ = psum.tile([P, 512], F32, name="ct", tag="tp", bufs=TPB)
+            for t in range(4):
+                c0 = 512 * gr + P * t
+                nc.tensor.transpose(t_[:, P * t : P * t + P], catn[i][:, c0 : c0 + P], ident[:])
+            cts[(i, gr)] = t_
+
+        def mul(i, gr):
+            b, ii = i // 4, i % 4
+            if (gr, b) not in hin:
+                hin[(gr, b)] = grp.tile([P, 2048], BF16, name="hin", tag="xh", align_bytes=64)
+            nc.vector.tensor_tensor(
+                out=hin[(gr, b)][:, 512 * ii : 512 * ii + 512].rearrange("p (r t) -> p r t", t=4),
+                in0=gate[(b, gr)][:, :, P * ii : P * ii + P].rearrange("p t r -> p r t"),
+                in1=cts[(i, gr)][:].rearrange("p (t r) -> p r t", t=4),
+                op=ALU.mult,
+            )
+
+        def hQ(gr, b, lo=0, n=512):
+            quantise(hq[(gr, b)], hin[(gr, b)], lo, n)
+
+        ots = {}
+
+        ps2 = {}
+
+        def s2p(i, h):
+            b, ii = i // 4, i % 4
+            ps = psum.tile([P, 512], F32, name="ps2", tag="s2", bufs=S2B)
+            for g in range(2):
+                nc.tensor.matmul_mx(
+                    out=ps[:],
+                    lhsT=hq[(g, b)][0][:, P * ii : P * ii + P].bitcast(FP8X4),
+                    lhsT_scale=hq[(g, b)][1][:, P * ii : P * ii + P],
+                    rhs=wq[("wo", g, h)][0][:].bitcast(FP8X4),
+                    rhs_scale=wq[("wo", g, h)][1][:],
+                    start=(g == 0),
+                    stop=(g == 1),
+                )
+            ps2[(i, h)] = ps
+
+        def oslice(i, h):
+            if i not in ots:
+                ots[i] = outp.tile([P, 1024], F32, name="ot")
+            return ots[i][:, 512 * h : 512 * h + 512]
+
+        def s2e(i, h):
+            nc.vector.tensor_tensor(out=oslice(i, h), in0=ps2[(i, h)][:], in1=bo_bc[:, 512 * h : 512 * h + 512], op=ALU.add)
+
+        def s2c(i, h):
+            nc.scalar.copy(out=oslice(i, h), in_=ps2[(i, h)][:])
+
+        def s2g(i, h):
+            nc.gpsimd.tensor_tensor(out=oslice(i, h), in0=oslice(i, h), in1=bo_bc[:, 512 * h : 512 * h + 512], op=ALU.add)
+
+        def st_(i):
+            nc.sync.dma_start(out=ov[:, i, :], in_=ots[i][:])
+
+        HQW = 512
+        consts()
+        bias()
+        ld_r(2)
+        ld_r(3)
+        ld_x(1)
+        ld_x(0)
+        ld_r(1)
+        ld_r(0)
+        ld_wg(0)
+        ld_r(6)
+        ld_r(5)
+        bn(2)
+        ld_r(4)
+        ld_r(7)
+        bn(3)
+        xTp(3)
+        ld_wg(1)
+        xTp(2)
+        xTs(3)
+        cmb(1)
+        xTs(2)
+        xTp(0)
+        ld_x(3)
+        sq(1)
+        xTs(0)
+        xTp(1)
+        fin(1)
+        ld_x(2)
+        bn(1)
+        xTs(1)
+        ld_wo(0)
+        nrm(2)
+        bn(0)
+        nrm(3)
+        ct(2, 1)
+        cmb(0)
+        rg("G", "wg", 0, 0)
+        ld_wo(1)
+        bn(6)
+        sq(0)
+        rg("S", "wg", 0, 1)
+        xQ(0, 0)
+        fin(0)
+        bn(4)
+        nrm(1)
+        bn(5)
+        nrm(0)
+        rg("G", "wg", 1, 0)
+        xQ(1, 0)
+        rg("S", "wg", 1, 1)
+        bn(7)
+        xTp(7)
+        wQ("wg", 0, 0)
+        xTp(5)
+        ct(3, 1)
+        wQ("wg", 1, 0)
+        xTs(7)
+        wQ("wg", 0, 1)
+        xTs(5)
+        xTp(4)
+        cmb(2)
+        xTs(4)
+        xTp(6)
+        s1p(0, 1)
+        cmb(3)
+        rg("G", "wo", 0, 1)
+        xTs(6)
+        wQ("wg", 1, 1)
+        sq(2)
+        sq(3)
+        s1a(0, 1)
+        fin(2)
+        fin(3)
+        s1p(0, 6)
+        xQ(0, 1)
+        s1p(0, 4)
+        ct(2, 0)
+        rg("G", "wo", 1, 1)
+        wQ("wo", 0, 1)
+        s1a(0, 6)
+        s1p(0, 2)
+        xQ(1, 1)
+        s1a(0, 4)
+        s1p(0, 7)
+        s1a(0, 2)
+        s1p(0, 5)
+        s1a(0, 7)
+        s1p(0, 3)
+        s1a(0, 5)
+        s1p(0, 0)
+        rg("G", "wo", 1, 0)
+        wQ("wo", 1, 1)
+        s1a(0, 3)
+        s1p(1, 6)
+        mul(2, 1)
+        s1a(0, 0)
+        s1p(1, 1)
+        mul(3, 1)
+        s1a(1, 6)
+        ct(3, 0)
+        mul(2, 0)
+        ct(0, 1)
+        s1a(1, 1)
+        mul(3, 0)
+        ct(0, 0)
+        rg("G", "wo", 0, 0)
+        nrm(6)
+        mul(0, 1)
+        ct(1, 1)
+        s1p(1, 3)
+        wQ("wo", 1, 0)
+        s1p(1, 0)
+        mul(1, 1)
+        nrm(5)
+        s1p(1, 2)
+        mul(0, 0)
+        ct(1, 0)
+        hQ(1, 0, HQW * 0, HQW)
+        s1a(1, 3)
+        ct(6, 0)
+        mul(1, 0)
+        ct(5, 0)
+        s1a(1, 0)
+        s1p(1, 5)
+        wQ("wo", 0, 0)
+        s1a(1, 2)
+        s1p(1, 4)
+        hQ(0, 0, HQW * 0, HQW)
+        s1p(1, 7)
+        mul(5, 0)
+        s1a(1, 4)
+        s2p(1, 0)
+        mul(6, 0)
+        s1a(1, 7)
+        s2p(0, 0)
+        s2e(1, 0)
+        s1a(1, 5)
+        ct(5, 1)
+        s2e(0, 0)
+        nrm(7)
+        s2p(1, 1)
+        mul(5, 1)
+        s2p(0, 1)
+        s2e(1, 1)
+        nrm(4)
+        ct(7, 0)
+        s2e(0, 1)
+        ct(7, 1)
+        mul(7, 0)
+        st_(0)
+        st_(1)
+        ct(4, 1)
+        mul(7, 1)
+        ct(6, 1)
+        mul(4, 1)
+        ct(4, 0)
+        s2p(3, 1)
+        mul(6, 1)
+        s2p(2, 1)
+        mul(4, 0)
+        s2e(3, 1)
+        hQ(0, 1, HQW * 0, HQW)
+        s2p(2, 0)
+        s2e(2, 1)
+        s2e(2, 0)
+        s2p(3, 0)
+        hQ(1, 1, HQW * 0, HQW)
+        st_(2)
+        s2e(3, 0)
+        s2p(4, 1)
+        st_(3)
+        s2p(5, 1)
+        s2e(4, 1)
+        s2e(5, 1)
+        s2p(4, 0)
+        s2p(6, 0)
+        s2e(4, 0)
+        s2p(5, 0)
+        st_(4)
+        s2e(6, 0)
+        s2e(5, 0)
+        s2p(6, 1)
+        s2p(7, 1)
+        st_(5)
+        s2e(6, 1)
+        s2e(7, 1)
+        s2p(7, 0)
+        st_(6)
+        s2e(7, 0)
+        st_(7)

@@ -195,7 +195,14 @@ def tile_gatedmultiscaleretentionlayer_pa_kernel(tc, x, ret_cat, Wg, bg, Wo, bo,
             elif eng == "S":
                 nc.scalar.copy(out=dst, in_=s)
             else:
-                nc.gpsimd.tensor_scalar(out=dst, in0=s, scalar1=1.0, scalar2=0.0, op0=ALU.mult, op1=ALU.add)
+                nc.gpsimd.tensor_scalar(
+                    out=t[:].rearrange("p (n t) -> p n t", t=4),
+                    in0=w_raw[(w, g)][:, :, 512 * h : 512 * h + 512].rearrange("p t n -> p n t"),
+                    scalar1=1.0,
+                    scalar2=0.0,
+                    op0=ALU.mult,
+                    op1=ALU.add,
+                )
             win[(w, g, h)] = t
 
         def wQ(w, g, h):

@@ -19,9 +19,6 @@ EPS = 1e-5
 PIN = True
 GRPBUFS = 4
 OUTBUFS = 4
-TPB = 3
-S1B = 3
-S2B = 2
 
 
 def tile_gatedmultiscaleretentionlayer_pa_kernel(tc, x, ret_cat, Wg, bg, Wo, bo, out):
@@ -49,6 +46,7 @@ def tile_gatedmultiscaleretentionlayer_pa_kernel(tc, x, ret_cat, Wg, bg, Wo, bo,
         ones = const.tile([P, P], BF16, name="ones")
         epst = const.tile([P, 1], F32, name="epst")
         warm = const.tile([P, 1], F32, name="warm")
+        mhalf = const.tile([P, 16], F32, name="mhalf")
         bgf = const.tile([P, P], F32, name="bgf")
         bgT = const.tile([P, 8], F32, name="bgT")
         bo_bc = const.tile([P, 1024], F32, name="bo_bc")
@@ -59,17 +57,21 @@ def tile_gatedmultiscaleretentionlayer_pa_kernel(tc, x, ret_cat, Wg, bg, Wo, bo,
             nc.vector.memset(bopad[:], 0.0)
             nc.vector.memset(ones[:], 1.0)
             nc.vector.memset(epst[:], 1.0)
+            nc.vector.memset(mhalf[:], -0.5)
             nc.scalar.dma_start(out=bgpad[0:8, :], in_=bg.rearrange("(c p) -> c p", p=P))
             nc.scalar.dma_start(out=bopad[0:1, :], in_=bo.rearrange("(o d) -> o d", o=1))
             nc.scalar.activation(out=warm[:], in_=epst[:], func=ACT.Sqrt)
 
+        def bank(k):
+            return psum.tile([P, 512], F32, name="bank%d" % k, tag="bank%d" % k)
+
         def bias():
             nc.vector.tensor_copy(out=bgf[:], in_=bgpad[:])
-            pb = psum.tile([P, 512], F32, name="pb", tag="s2", bufs=S2B)
+            pb = bank(0)
             nc.tensor.transpose(pb[:, 0:P], bgf[:], ident[:])
             nc.vector.tensor_copy(out=bgT[:], in_=pb[:, 0:8])
             for h in range(2):
-                pbo = psum.tile([P, 512], F32, name="pbo", tag="s2", bufs=S2B)
+                pbo = bank(1 + h)
                 nc.tensor.matmul(pbo[:], lhsT=ones[:], rhs=bopad[:, 512 * h : 512 * h + 512], start=True, stop=True)
                 nc.scalar.copy(out=bo_bc[:, 512 * h : 512 * h + 512], in_=pbo[:])
 
@@ -89,10 +91,14 @@ def tile_gatedmultiscaleretentionlayer_pa_kernel(tc, x, ret_cat, Wg, bg, Wo, bo,
                 in_=Wg[512 * g : 512 * g + 512, :].rearrange("(u p e) n -> p u (e n)", u=2, e=2),
             )
 
-        def ld_wo(g):
+        def ld_wo(g, h):
             nc.sync.dma_start(
-                out=w_raw[("wo", g)][:], in_=Wo[512 * g : 512 * g + 512, :].rearrange("(t p) n -> p t n", p=P)
+                out=w_raw[("wo", g)][:, :, 512 * h : 512 * h + 512],
+                in_=Wo[512 * g : 512 * g + 512, 512 * h : 512 * h + 512].rearrange("(t p) n -> p t n", p=P),
             )
+
+        def silu_table():
+            nc.scalar.activation(out=warm[:], in_=epst[:], func=ACT.Silu)
 
         def mx_tiles(nm, width):
             return (
@@ -115,35 +121,70 @@ def tile_gatedmultiscaleretentionlayer_pa_kernel(tc, x, ret_cat, Wg, bg, Wo, bo,
         sm = [stat.tile([P, 16, 2], F32, name="sm%d" % j) for j in range(4)]
         sd = [stat.tile([P, 16], F32, name="sd%d" % j) for j in range(4)]
 
-        def bn(i):
+        def bn(i, short=()):
             for h in range(8):
                 nc.vector.bn_stats(out=st[i // 2][:, 8 * (i % 2) + h, :], in_=r_raw[i][:, P * h : P * h + P])
+                if h % 2 == 0 and h // 2 < len(short):
+                    short[h // 2]()
+            for f in short[4:]:
+                f()
 
         vv = {}
 
+        def weave(long_ops, short):
+            for k, f in enumerate(long_ops):
+                f()
+                if k < len(short):
+                    short[k]()
+            for f in short[len(long_ops) :]:
+                f()
+
         def cmb(j):
-            nc.vector.tensor_reduce(
-                out=sm[j][:], in_=st[j][:].rearrange("p n (a k) -> p n k a", a=2)[:, :, 1:3, :], axis=AX.X, op=ALU.add
-            )
             d = stat.tile([P, 16], F32, name="d%d" % j)
-            nc.vector.tensor_tensor(out=d[:], in0=st[j][:, :, 1], in1=st[j][:, :, 4], op=ALU.subtract)
             d2 = stat.tile([P, 16], F32, name="dd%d" % j)
-            nc.vector.tensor_tensor(out=d2[:], in0=d[:], in1=d[:], op=ALU.mult)
             v = stat.tile([P, 16], F32, name="v%d" % j)
-            nc.vector.scalar_tensor_tensor(out=v[:], in0=d2[:], scalar=32.0, in1=sm[j][:, :, 1], op0=ALU.mult, op1=ALU.add)
             ve = stat.tile([P, 16], F32, name="ve%d" % j)
-            nc.vector.tensor_scalar(out=ve[:], in0=v[:], scalar1=1.0 / 128.0, scalar2=EPS, op0=ALU.mult, op1=ALU.add)
+
             vv[j] = ve
+            return [
+                lambda: nc.vector.tensor_tensor(out=d[:], in0=st[j][:, :, 1], in1=st[j][:, :, 4], op=ALU.subtract),
+                lambda: nc.vector.tensor_reduce(
+                    out=sm[j][:], in_=st[j][:].rearrange("p n (a k) -> p n k a", a=2)[:, :, 1:3, :], axis=AX.X, op=ALU.add
+                ),
+                lambda: nc.vector.tensor_tensor(out=d2[:], in0=d[:], in1=d[:], op=ALU.mult),
+                lambda: nc.vector.scalar_tensor_tensor(
+                    out=v[:], in0=d2[:], scalar=32.0, in1=sm[j][:, :, 1], op0=ALU.mult, op1=ALU.add
+                ),
+                lambda: nc.vector.tensor_scalar(
+                    out=ve[:], in0=v[:], scalar1=1.0 / 128.0, scalar2=EPS, op0=ALU.mult, op1=ALU.add
+                ),
+            ]
 
         def sq(j):
-            nc.scalar.activation(out=sd[j][:], in_=vv[j][:], func=ACT.Sqrt)
+            if j in POW:
+                nc.gpsimd.tensor_tensor(out=rstd[:, 16 * j : 16 * j + 16], in0=vv[j][:], in1=mhalf[:], op=ALU.pow)
+            else:
+                nc.scalar.activation(out=sd[j][:], in_=vv[j][:], func=ACT.Sqrt)
+
+        dealt = [0]
+
+        def drip(todo):
+            if dealt[0] < len(todo):
+                todo[dealt[0]]()
+                dealt[0] += 1
+
+        def flush(todo):
+            for f in todo[dealt[0] :]:
+                f()
+            dealt[0] = len(todo)
 
         def fin(j):
             cols = slice(16 * j, 16 * j + 16)
-            nc.vector.reciprocal(out=rstd[:, cols], in_=sd[j][:])
-            nc.vector.scalar_tensor_tensor(
-                out=nmr[:, cols], in0=sm[j][:, :, 0], scalar=-0.5, in1=rstd[:, cols], op0=ALU.mult, op1=ALU.mult
-            )
+            return ([] if j in POW else [lambda: nc.vector.reciprocal(out=rstd[:, cols], in_=sd[j][:])]) + [
+                lambda: nc.vector.scalar_tensor_tensor(
+                    out=nmr[:, cols], in0=sm[j][:, :, 0], scalar=-0.5, in1=rstd[:, cols], op0=ALU.mult, op1=ALU.mult
+                ),
+            ]
 
         catn = {}
 
@@ -164,9 +205,9 @@ def tile_gatedmultiscaleretentionlayer_pa_kernel(tc, x, ret_cat, Wg, bg, Wo, bo,
 
         xts = {}
 
-        def xTp(i):
+        def xTp(i, k):
             xw = x_raw[i // 2][:, i % 2, :].bitcast(F32)
-            xt = psum.tile([P, 512], F32, name="xt", tag="s2", bufs=S2B)
+            xt = bank(k)
             for w in range(4):
                 nc.tensor.transpose(xt[:, P * w : P * w + P], xw[:, P * w : P * w + P], ident[:])
             xts[i] = xt
@@ -212,9 +253,9 @@ def tile_gatedmultiscaleretentionlayer_pa_kernel(tc, x, ret_cat, Wg, bg, Wo, bo,
 
         ps1 = {}
 
-        def s1p(b, c):
+        def s1p(b, c, k):
             gr, t = c // 4, c % 4
-            ps = psum.tile([P, 512], F32, name="ps1", tag="s1", bufs=S1B)
+            ps = bank(k)
             for g in range(2):
                 cq, cs = wq[("wg", g, gr)]
                 nc.tensor.matmul_mx(
@@ -239,8 +280,8 @@ def tile_gatedmultiscaleretentionlayer_pa_kernel(tc, x, ret_cat, Wg, bg, Wo, bo,
         hin = {}
         cts = {}
 
-        def ct(i, gr):
-            t_ = psum.tile([P, 512], F32, name="ct", tag="tp", bufs=TPB)
+        def ct(i, gr, k):
+            t_ = bank(k)
             for t in range(4):
                 c0 = 512 * gr + P * t
                 nc.tensor.transpose(t_[:, P * t : P * t + P], catn[i][:, c0 : c0 + P], ident[:])
@@ -264,9 +305,9 @@ def tile_gatedmultiscaleretentionlayer_pa_kernel(tc, x, ret_cat, Wg, bg, Wo, bo,
 
         ps2 = {}
 
-        def s2p(i, h):
+        def s2p(i, h, k):
             b, ii = i // 4, i % 4
-            ps = psum.tile([P, 512], F32, name="ps2", tag="s2", bufs=S2B)
+            ps = bank(k)
             for g in range(2):
                 nc.tensor.matmul_mx(
                     out=ps[:],
@@ -296,194 +337,204 @@ def tile_gatedmultiscaleretentionlayer_pa_kernel(tc, x, ret_cat, Wg, bg, Wo, bo,
         def st_(i):
             nc.sync.dma_start(out=ov[:, i, :], in_=ots[i][:])
 
-        HQW = 512
+        HQW = 256
+        POW = (3,)
         consts()
         bias()
-        ld_r(2)
-        ld_r(3)
-        ld_x(1)
-        ld_x(0)
         ld_r(1)
         ld_r(0)
-        ld_wg(0)
-        ld_r(6)
-        ld_r(5)
-        bn(2)
+        ld_r(2)
+        ld_x(1)
         ld_r(4)
-        ld_r(7)
-        bn(3)
-        xTp(3)
-        ld_wg(1)
-        xTp(2)
-        xTs(3)
-        cmb(1)
-        xTs(2)
-        xTp(0)
-        ld_x(3)
-        sq(1)
-        xTs(0)
-        xTp(1)
-        fin(1)
+        ld_x(0)
+        ld_r(3)
         ld_x(2)
+        ld_wg(0)
         bn(1)
-        xTs(1)
-        ld_wo(0)
-        nrm(2)
+        ld_r(5)
+        ld_r(6)
         bn(0)
-        nrm(3)
-        ct(2, 1)
-        cmb(0)
-        rg("G", "wg", 0, 0)
-        ld_wo(1)
-        bn(6)
+        ld_wg(1)
+        xTp(3, 0)
+        ld_wo(0, 1)
+        xTp(2, 1)
+        bn(2, cmb(0))
+        ld_x(3)
+        xTs(2)
+        xTs(3)
+        xTp(1, 2)
+        ld_r(7)
+        xTp(0, 3)
+        ld_wo(1, 1)
         sq(0)
+        xTs(1)
+        bn(3, fin(0))
+        xTs(0)
+        xTp(4, 4)
+        ld_wo(0, 0)
+        xTp(5, 5)
+        xTs(4)
+        bn(4, cmb(1))
+        nrm(1)
+        rg("G", "wg", 0, 0)
+        ld_wo(1, 0)
+        xTs(5)
+        xQ(1, 0)
+        sq(1)
         rg("S", "wg", 0, 1)
         xQ(0, 0)
-        fin(0)
-        bn(4)
-        nrm(1)
-        bn(5)
+        bn(5, fin(1))
         nrm(0)
-        rg("G", "wg", 1, 0)
-        xQ(1, 0)
-        rg("S", "wg", 1, 1)
-        bn(7)
-        xTp(7)
         wQ("wg", 0, 0)
-        xTp(5)
-        ct(3, 1)
-        wQ("wg", 1, 0)
-        xTs(7)
+        rg("G", "wg", 1, 0)
+        rg("V", "wg", 1, 1)
+        nrm(2)
         wQ("wg", 0, 1)
-        xTs(5)
-        xTp(4)
-        cmb(2)
-        xTs(4)
-        xTp(6)
-        s1p(0, 1)
-        cmb(3)
-        rg("G", "wo", 0, 1)
-        xTs(6)
         wQ("wg", 1, 1)
+        nrm(3)
+        xTp(7, 6)
+        bn(6, cmb(2))
+        xTp(6, 7)
+        rg("G", "wo", 0, 1)
+        s1p(0, 7, 1)
+        xTs(6)
+        ct(0, 0, 0)
+        xTs(7)
+        wQ("wg", 1, 0)
+        ct(2, 0, 2)
+        ct(1, 0, 3)
         sq(2)
-        sq(3)
-        s1a(0, 1)
-        fin(2)
-        fin(3)
-        s1p(0, 6)
-        xQ(0, 1)
-        s1p(0, 4)
-        ct(2, 0)
-        rg("G", "wo", 1, 1)
-        wQ("wo", 0, 1)
-        s1a(0, 6)
-        s1p(0, 2)
-        xQ(1, 1)
-        s1a(0, 4)
-        s1p(0, 7)
-        s1a(0, 2)
-        s1p(0, 5)
         s1a(0, 7)
-        s1p(0, 3)
-        s1a(0, 5)
-        s1p(0, 0)
-        rg("G", "wo", 1, 0)
-        wQ("wo", 1, 1)
+        xQ(1, 1)
+        s1p(0, 2, 4)
+        rg("G", "wo", 1, 1)
+        bn(7, fin(2))
+        s1p(0, 3, 5)
+        s1p(0, 0, 7)
         s1a(0, 3)
-        s1p(1, 6)
-        mul(2, 1)
+        wQ("wo", 0, 1)
+        s1p(0, 1, 6)
+        s1a(0, 2)
+        s1p(0, 5, 1)
+        xQ(0, 1)
         s1a(0, 0)
-        s1p(1, 1)
-        mul(3, 1)
-        s1a(1, 6)
-        ct(3, 0)
-        mul(2, 0)
-        ct(0, 1)
-        s1a(1, 1)
-        mul(3, 0)
-        ct(0, 0)
+        s1p(0, 6, 5)
         rg("G", "wo", 0, 0)
-        nrm(6)
-        mul(0, 1)
-        ct(1, 1)
-        s1p(1, 3)
-        wQ("wo", 1, 0)
-        s1p(1, 0)
-        mul(1, 1)
-        nrm(5)
-        s1p(1, 2)
+        s1p(0, 4, 4)
+        s1a(0, 1)
+        wQ("wo", 1, 1)
+        s1p(1, 5, 7)
+        s1a(0, 6)
+        c3 = cmb(3)
         mul(0, 0)
-        ct(1, 0)
-        hQ(1, 0, HQW * 0, HQW)
-        s1a(1, 3)
-        ct(6, 0)
+        drip(c3)
+        ct(2, 1, 6)
+        s1a(0, 4)
         mul(1, 0)
-        ct(5, 0)
-        s1a(1, 0)
-        s1p(1, 5)
-        wQ("wo", 0, 0)
-        s1a(1, 2)
-        s1p(1, 4)
+        drip(c3)
+        ct(1, 1, 5)
+        s1a(0, 5)
+        ct(0, 1, 0)
+        mul(2, 0)
+        drip(c3)
+        ct(3, 0, 4)
+        nrm(5)
+        rg("G", "wo", 1, 0)
+        ct(3, 1, 3)
         hQ(0, 0, HQW * 0, HQW)
-        s1p(1, 7)
-        mul(5, 0)
+        drip(c3)
+        s1p(1, 4, 1)
+        mul(0, 1)
+        drip(c3)
+        mul(1, 1)
+        drip(c3)
+        s1p(1, 6, 2)
         s1a(1, 4)
-        s2p(1, 0)
-        mul(6, 0)
-        s1a(1, 7)
-        s2p(0, 0)
-        s2e(1, 0)
-        s1a(1, 5)
-        ct(5, 1)
-        s2e(0, 0)
-        nrm(7)
-        s2p(1, 1)
-        mul(5, 1)
-        s2p(0, 1)
-        s2e(1, 1)
+        wQ("wo", 0, 0)
+        drip(c3)
+        s1p(1, 1, 0)
+        s1a(1, 6)
+        mul(3, 1)
+        drip(c3)
+        s1p(1, 3, 5)
         nrm(4)
-        ct(7, 0)
+        flush(c3)
+        sq(3)
+        hQ(1, 0, HQW * 0, HQW)
+        s1p(1, 2, 1)
+        mul(3, 0)
+        s1p(1, 7, 2)
+        wQ("wo", 1, 0)
+        s2p(1, 1, 3)
+        s1a(1, 2)
+        mul(2, 1)
+        s2p(0, 1, 4)
+        s1a(1, 5)
+        hQ(0, 0, HQW * 1, HQW)
+        s2p(0, 0, 1)
+        s2e(1, 1)
+        s1a(1, 3)
+        ct(4, 1, 6)
+        hQ(1, 0, HQW * 1, HQW)
+        s1a(1, 7)
         s2e(0, 1)
-        ct(7, 1)
-        mul(7, 0)
-        st_(0)
-        st_(1)
-        ct(4, 1)
-        mul(7, 1)
-        ct(6, 1)
+        s1p(1, 0, 7)
+        s1a(1, 1)
+        s2e(0, 0)
+        ct(5, 1, 3)
+        weave([], fin(3))
+        s1a(1, 0)
         mul(4, 1)
-        ct(4, 0)
-        s2p(3, 1)
-        mul(6, 1)
-        s2p(2, 1)
+        ct(5, 0, 5)
+        st_(0)
+        ct(4, 0, 2)
+        nrm(6)
+        mul(5, 1)
+        s2p(3, 0, 4)
+        mul(5, 0)
+        s2p(2, 1, 0)
         mul(4, 0)
-        s2e(3, 1)
-        hQ(0, 1, HQW * 0, HQW)
-        s2p(2, 0)
-        s2e(2, 1)
-        s2e(2, 0)
-        s2p(3, 0)
-        hQ(1, 1, HQW * 0, HQW)
-        st_(2)
+        nrm(7)
+        s2p(1, 0, 1)
         s2e(3, 0)
-        s2p(4, 1)
+        s2p(3, 1, 7)
+        hQ(1, 1, HQW * 0, HQW)
+        s2e(1, 0)
+        ct(7, 1, 6)
+        hQ(0, 1, HQW * 0, HQW)
+        ct(6, 0, 3)
+        s2e(2, 1)
+        ct(7, 0, 5)
+        s2e(3, 1)
+        s2p(5, 1, 2)
+        mul(6, 0)
+        ct(6, 1, 4)
         st_(3)
-        s2p(5, 1)
+        st_(1)
+        mul(7, 1)
+        s2p(2, 0, 1)
+        mul(6, 1)
+        s2p(4, 0, 0)
+        mul(7, 0)
+        s2p(4, 1, 7)
+        s2e(2, 0)
+        s2p(5, 0, 3)
+        hQ(1, 1, HQW * 1, HQW)
+        hQ(0, 1, HQW * 1, HQW)
+        st_(2)
         s2e(4, 1)
-        s2e(5, 1)
-        s2p(4, 0)
-        s2p(6, 0)
+        s2p(7, 0, 6)
         s2e(4, 0)
-        s2p(5, 0)
+        s2p(7, 1, 4)
+        s2e(7, 0)
         st_(4)
-        s2e(6, 0)
+        s2p(6, 1, 5)
+        s2e(7, 1)
+        s2p(6, 0, 1)
         s2e(5, 0)
-        s2p(6, 1)
-        s2p(7, 1)
+        st_(7)
+        s2e(5, 1)
+        s2e(6, 0)
         st_(5)
         s2e(6, 1)
-        s2e(7, 1)
-        s2p(7, 0)
         st_(6)
-        s2e(7, 0)
-        st_(7)

@@ -341,200 +341,197 @@ def tile_gatedmultiscaleretentionlayer_pa_kernel(tc, x, ret_cat, Wg, bg, Wo, bo,
         POW = (3,)
         consts()
         bias()
-        ld_r(1)
+        ld_wg(0)
         ld_r(0)
+        ld_r(1)
+        ld_x(3)
         ld_r(2)
         ld_x(1)
-        ld_r(4)
-        ld_x(0)
         ld_r(3)
-        ld_x(2)
-        ld_wg(0)
-        bn(1)
-        ld_r(5)
-        ld_r(6)
-        bn(0)
+        ld_x(0)
+        ld_r(4)
+        rg("S", "wg", 0, 1)
         ld_wg(1)
-        xTp(3, 0)
-        ld_wo(0, 1)
-        xTp(2, 1)
-        bn(2, cmb(0))
-        ld_x(3)
-        xTs(2)
-        xTs(3)
-        xTp(1, 2)
-        ld_r(7)
-        xTp(0, 3)
+        bn(0)
+        ld_x(2)
+        ld_r(5)
+        bn(1)
+        rg("S", "wg", 0, 0)
+        xTp(7, 0)
+        ld_wo(1, 0)
         ld_wo(1, 1)
+        bn(2, cmb(0))
+        xTp(2, 1)
+        ld_r(6)
+        xTs(7)
+        xTp(3, 2)
+        xTp(6, 3)
+        ld_wo(0, 1)
+        xTs(2)
+        wQ("wg", 0, 0)
         sq(0)
-        xTs(1)
+        xTs(6)
+        xTp(0, 4)
         bn(3, fin(0))
-        xTs(0)
-        xTp(4, 4)
+        ld_r(7)
+        xTs(3)
+        xTp(1, 5)
         ld_wo(0, 0)
-        xTp(5, 5)
-        xTs(4)
+        xTs(0)
+        xTs(1)
         bn(4, cmb(1))
         nrm(1)
-        rg("G", "wg", 0, 0)
-        ld_wo(1, 0)
+        nrm(0)
+        rg("V", "wg", 1, 0)
+        xTp(4, 6)
+        xTp(5, 7)
+        xQ(0, 0)
+        sq(1)
+        xTs(4)
+        wQ("wg", 1, 0)
         xTs(5)
         xQ(1, 0)
-        sq(1)
-        rg("S", "wg", 0, 1)
-        xQ(0, 0)
+        rg("S", "wo", 1, 0)
         bn(5, fin(1))
-        nrm(0)
-        wQ("wg", 0, 0)
-        rg("G", "wg", 1, 0)
+        s1p(0, 2, 0)
+        s1p(0, 0, 1)
         rg("V", "wg", 1, 1)
-        nrm(2)
-        wQ("wg", 0, 1)
-        wQ("wg", 1, 1)
+        s1p(0, 1, 3)
         nrm(3)
-        xTp(7, 6)
+        s1p(0, 3, 2)
         bn(6, cmb(2))
-        xTp(6, 7)
-        rg("G", "wo", 0, 1)
-        s1p(0, 7, 1)
-        xTs(6)
-        ct(0, 0, 0)
-        xTs(7)
-        wQ("wg", 1, 0)
-        ct(2, 0, 2)
-        ct(1, 0, 3)
+        nrm(2)
+        wQ("wg", 1, 1)
         sq(2)
-        s1a(0, 7)
         xQ(1, 1)
-        s1p(0, 2, 4)
-        rg("G", "wo", 1, 1)
-        bn(7, fin(2))
-        s1p(0, 3, 5)
-        s1p(0, 0, 7)
-        s1a(0, 3)
-        wQ("wo", 0, 1)
-        s1p(0, 1, 6)
-        s1a(0, 2)
-        s1p(0, 5, 1)
-        xQ(0, 1)
-        s1a(0, 0)
-        s1p(0, 6, 5)
-        rg("G", "wo", 0, 0)
-        s1p(0, 4, 4)
         s1a(0, 1)
-        wQ("wo", 1, 1)
-        s1p(1, 5, 7)
-        s1a(0, 6)
+        ct(2, 0, 4)
+        wQ("wg", 0, 1)
+        ct(1, 0, 5)
+        xQ(0, 1)
+        s1p(0, 6, 6)
+        bn(7, fin(2))
+        s1a(0, 2)
+        s1p(0, 7, 7)
+        s1a(0, 3)
+        s1p(0, 5, 3)
+        s1a(0, 0)
+        ct(3, 1, 0)
         c3 = cmb(3)
-        mul(0, 0)
+        wQ("wo", 1, 0)
         drip(c3)
-        ct(2, 1, 6)
-        s1a(0, 4)
+        ct(3, 0, 2)
+        s1a(0, 5)
+        s1p(0, 4, 1)
         mul(1, 0)
         drip(c3)
-        ct(1, 1, 5)
-        s1a(0, 5)
-        ct(0, 1, 0)
-        mul(2, 0)
+        s1a(0, 6)
+        mul(3, 0)
         drip(c3)
-        ct(3, 0, 4)
-        nrm(5)
-        rg("G", "wo", 1, 0)
-        ct(3, 1, 3)
-        hQ(0, 0, HQW * 0, HQW)
-        drip(c3)
-        s1p(1, 4, 1)
-        mul(0, 1)
-        drip(c3)
-        mul(1, 1)
-        drip(c3)
-        s1p(1, 6, 2)
-        s1a(1, 4)
-        wQ("wo", 0, 0)
-        drip(c3)
-        s1p(1, 1, 0)
-        s1a(1, 6)
-        mul(3, 1)
+        s1p(1, 2, 3)
+        s1a(0, 7)
+        rg("V", "wo", 1, 1)
         drip(c3)
         s1p(1, 3, 5)
-        nrm(4)
+        s1a(0, 4)
+        ct(0, 1, 6)
+        rg("S", "wo", 0, 0)
+        ct(2, 1, 2)
+        mul(2, 0)
+        drip(c3)
+        ct(1, 1, 7)
         flush(c3)
         sq(3)
-        hQ(1, 0, HQW * 0, HQW)
-        s1p(1, 2, 1)
-        mul(3, 0)
-        s1p(1, 7, 2)
-        wQ("wo", 1, 0)
-        s2p(1, 1, 3)
-        s1a(1, 2)
+        mul(0, 1)
+        s1p(1, 1, 1)
+        mul(3, 1)
+        ct(0, 0, 4)
         mul(2, 1)
-        s2p(0, 1, 4)
-        s1a(1, 5)
+        s1p(1, 5, 6)
+        rg("S", "wo", 0, 1)
         hQ(0, 0, HQW * 1, HQW)
-        s2p(0, 0, 1)
-        s2e(1, 1)
-        s1a(1, 3)
-        ct(4, 1, 6)
+        s1p(1, 4, 0)
+        mul(0, 0)
+        s1p(1, 0, 2)
         hQ(1, 0, HQW * 1, HQW)
-        s1a(1, 7)
-        s2e(0, 1)
-        s1p(1, 0, 7)
-        s1a(1, 1)
-        s2e(0, 0)
-        ct(5, 1, 3)
+        wQ("wo", 0, 0)
+        s1p(1, 7, 4)
+        wQ("wo", 1, 1)
+        s1a(1, 3)
+        wQ("wo", 0, 1)
+        s1a(1, 2)
+        s2p(3, 0, 5)
+        mul(1, 1)
+        s1a(1, 5)
+        s2p(3, 1, 3)
         weave([], fin(3))
-        s1a(1, 0)
-        mul(4, 1)
-        ct(5, 0, 5)
-        st_(0)
-        ct(4, 0, 2)
-        nrm(6)
-        mul(5, 1)
-        s2p(3, 0, 4)
-        mul(5, 0)
-        s2p(2, 1, 0)
-        mul(4, 0)
-        nrm(7)
-        s2p(1, 0, 1)
+        hQ(0, 0, HQW * 0, HQW)
+        s1a(1, 1)
+        hQ(1, 0, HQW * 0, HQW)
+        s2p(2, 0, 7)
         s2e(3, 0)
-        s2p(3, 1, 7)
-        hQ(1, 1, HQW * 0, HQW)
-        s2e(1, 0)
-        ct(7, 1, 6)
-        hQ(0, 1, HQW * 0, HQW)
-        ct(6, 0, 3)
-        s2e(2, 1)
-        ct(7, 0, 5)
+        nrm(7)
+        s2p(0, 1, 6)
+        s2e(2, 0)
+        s2p(0, 0, 1)
+        nrm(4)
+        s2e(0, 1)
+        s1p(1, 6, 5)
+        s2e(0, 0)
+        s2p(2, 1, 7)
         s2e(3, 1)
-        s2p(5, 1, 2)
-        mul(6, 0)
-        ct(6, 1, 4)
+        s1a(1, 0)
+        s2p(1, 0, 6)
+        s2e(2, 1)
+        nrm(6)
+        ct(4, 0, 1)
+        s2e(1, 0)
+        ct(7, 0, 3)
+        st_(2)
+        ct(4, 1, 2)
         st_(3)
+        mul(4, 0)
+        st_(0)
+        s2p(1, 1, 7)
+        s1a(1, 4)
+        mul(7, 0)
+        ct(6, 0, 6)
+        s1a(1, 6)
+        s2e(1, 1)
+        ct(6, 1, 1)
+        s1a(1, 7)
+        ct(7, 1, 0)
+        mul(6, 0)
+        nrm(5)
         st_(1)
         mul(7, 1)
-        s2p(2, 0, 1)
         mul(6, 1)
-        s2p(4, 0, 0)
-        mul(7, 0)
-        s2p(4, 1, 7)
-        s2e(2, 0)
-        s2p(5, 0, 3)
-        hQ(1, 1, HQW * 1, HQW)
         hQ(0, 1, HQW * 1, HQW)
-        st_(2)
-        s2e(4, 1)
-        s2p(7, 0, 6)
-        s2e(4, 0)
-        s2p(7, 1, 4)
-        s2e(7, 0)
-        st_(4)
-        s2p(6, 1, 5)
+        ct(5, 0, 3)
+        hQ(1, 1, HQW * 1, HQW)
+        ct(5, 1, 5)
+        mul(4, 1)
+        s2p(7, 1, 7)
+        mul(5, 0)
+        mul(5, 1)
+        s2p(6, 1, 4)
         s2e(7, 1)
-        s2p(6, 0, 1)
-        s2e(5, 0)
-        st_(7)
-        s2e(5, 1)
-        s2e(6, 0)
-        st_(5)
+        s2p(7, 0, 6)
+        hQ(0, 1, HQW * 0, HQW)
+        s2p(6, 0, 0)
+        hQ(1, 1, HQW * 0, HQW)
+        s2e(7, 0)
+        s2p(5, 0, 1)
         s2e(6, 1)
+        st_(7)
+        s2p(5, 1, 2)
+        s2e(6, 0)
+        s2p(4, 0, 3)
+        s2e(5, 0)
         st_(6)
+        s2p(4, 1, 5)
+        s2e(5, 1)
+        s2e(4, 0)
+        st_(5)
+        s2e(4, 1)
+        st_(4)

@@ -15,523 +15,395 @@ ALU = mybir.AluOpType
 AX = mybir.AxisListType
 
 P = 128
+HEADS = 8
 EPS = 1e-5
-PIN = True
-GRPBUFS = 4
-OUTBUFS = 4
+BANKS = 8
+
+LOADS = (
+    ("r", 0), ("wg", 0, 0), ("r", 1), ("wg", 0, 1), ("r", 2), ("x", 0), ("x", 1), ("r", 3), ("wo", 0, 0), ("r", 4),
+    ("wg", 1, 0), ("x", 2), ("r", 5), ("x", 3), ("wg", 1, 1), ("wo", 1, 1), ("r", 6), ("r", 7), ("wo", 1, 0), ("wo", 0, 1),
+)
 
 
 def tile_gatedmultiscaleretentionlayer_pa_kernel(tc, x, ret_cat, Wg, bg, Wo, bo, out):
     nc = tc.nc
-    xv = x.flatten_outer_dims().rearrange("(p i) k -> p i k", i=8)
-    rv = ret_cat.flatten_outer_dims().rearrange("(p i) c -> p i c", i=8)
-    ov = out.flatten_outer_dims().rearrange("(p i) d -> p i d", i=8)
+    x_tiles = x.flatten_outer_dims().rearrange("(p i) k -> p i k", i=8)
+    r_tiles = ret_cat.flatten_outer_dims().rearrange("(p i) c -> p i c", i=8)
+    out_tiles = out.flatten_outer_dims().rearrange("(p i) d -> p i d", i=8)
 
     with ExitStack() as ctx:
         const = ctx.enter_context(tc.tile_pool(name="const", bufs=1))
         raw = ctx.enter_context(tc.tile_pool(name="raw", bufs=1))
-        grp = ctx.enter_context(tc.tile_pool(name="grp", bufs=GRPBUFS))
-        mxp = ctx.enter_context(tc.tile_pool(name="mxp", bufs=1))
+        grouped = ctx.enter_context(tc.tile_pool(name="grouped", bufs=1))
+        packed = ctx.enter_context(tc.tile_pool(name="packed", bufs=1))
         stat = ctx.enter_context(tc.tile_pool(name="stat", bufs=1))
-        catp = ctx.enter_context(tc.tile_pool(name="catp", bufs=8))
-        gatep = ctx.enter_context(tc.tile_pool(name="gatep", bufs=1))
-        outp = ctx.enter_context(tc.tile_pool(name="outp", bufs=OUTBUFS))
+        cat_pool = ctx.enter_context(tc.tile_pool(name="cat", bufs=8))
+        gate_pool = ctx.enter_context(tc.tile_pool(name="gate", bufs=1))
+        out_pool = ctx.enter_context(tc.tile_pool(name="out", bufs=4))
         psum = ctx.enter_context(tc.psum_pool(name="psum", bufs=1))
-        if PIN:
-            ctx.enter_context(tc.manual_schedule())
+        ctx.enter_context(tc.manual_schedule())
 
-        ident = const.tile([P, P], F32, name="ident")
-        bgpad = const.tile([P, P], BF16, name="bgpad")
-        bopad = const.tile([P, 1024], BF16, name="bopad")
+        banks_taken = [0]
+
+        def bank():
+            k = banks_taken[0] % BANKS
+            banks_taken[0] += 1
+            return psum.tile([P, 512], F32, name="bank%d" % k)
+
+        identity = const.tile([P, P], F32, name="identity")
+        make_identity(nc, identity[:])
+        bg_rows = const.tile([P, P], BF16, name="bg_rows")
+        nc.vector.memset(bg_rows[:], 0.0)
+        bo_row = const.tile([P, 1024], BF16, name="bo_row")
+        nc.vector.memset(bo_row[:], 0.0)
         ones = const.tile([P, P], BF16, name="ones")
-        epst = const.tile([P, 1], F32, name="epst")
-        warm = const.tile([P, 1], F32, name="warm")
-        mhalf = const.tile([P, 16], F32, name="mhalf")
-        bgf = const.tile([P, P], F32, name="bgf")
-        bgT = const.tile([P, 8], F32, name="bgT")
-        bo_bc = const.tile([P, 1024], F32, name="bo_bc")
+        nc.vector.memset(ones[:], 1.0)
+        minus_half = const.tile([P, 2 * HEADS], F32, name="minus_half")
+        nc.vector.memset(minus_half[:], -0.5)
+        nc.scalar.dma_start(out=bg_rows[0:HEADS, :], in_=bg.rearrange("(c p) -> c p", p=P))
+        nc.scalar.dma_start(out=bo_row[0:1, :], in_=bo.rearrange("(o d) -> o d", o=1))
+        scratch = const.tile([P, 1], F32, name="scratch")
+        nc.scalar.activation(out=scratch[:], in_=minus_half[:, 0:1], func=ACT.Silu)
 
-        def consts():
-            make_identity(nc, ident[:])
-            nc.vector.memset(bgpad[:], 0.0)
-            nc.vector.memset(bopad[:], 0.0)
-            nc.vector.memset(ones[:], 1.0)
-            nc.vector.memset(epst[:], 1.0)
-            nc.vector.memset(mhalf[:], -0.5)
-            nc.scalar.dma_start(out=bgpad[0:8, :], in_=bg.rearrange("(c p) -> c p", p=P))
-            nc.scalar.dma_start(out=bopad[0:1, :], in_=bo.rearrange("(o d) -> o d", o=1))
-            nc.scalar.activation(out=warm[:], in_=epst[:], func=ACT.Sqrt)
+        r_raw = [raw.tile([P, 1024], BF16, name="r_raw%d" % i) for i in range(8)]
+        x_raw = [raw.tile([P, 2, 1024], BF16, name="x_raw%d" % j) for j in range(4)]
+        w_raw = {(w, g): raw.tile([P, 4, 1024], BF16, name="%s_raw%d" % (w, g)) for w in ("wg", "wo") for g in range(2)}
 
-        def bank(k):
-            return psum.tile([P, 512], F32, name="bank%d" % k, tag="bank%d" % k)
+        def load(what, a, h=0):
+            cols = slice(512 * h, 512 * h + 512)
+            if what == "r":
+                nc.sync.dma_start(out=r_raw[a][:], in_=r_tiles[:, a, :])
+            elif what == "x":
+                nc.sync.dma_start(out=x_raw[a][:], in_=x_tiles[:, 2 * a : 2 * a + 2, :])
+            elif what == "wg":
+                for u in range(2):
+                    rows = slice(512 * a + 256 * u, 512 * a + 256 * u + 256)
+                    nc.sync.dma_start(
+                        out=w_raw[("wg", a)][:, 2 * u : 2 * u + 2, cols],
+                        in_=Wg[rows, cols].rearrange("(p e) n -> p e n", e=2),
+                    )
+            else:
+                nc.sync.dma_start(
+                    out=w_raw[("wo", a)][:, :, cols],
+                    in_=Wo[512 * a : 512 * a + 512, cols].rearrange("(t p) n -> p t n", p=P),
+                )
 
-        def bias():
-            nc.vector.tensor_copy(out=bgf[:], in_=bgpad[:])
-            pb = bank(0)
-            nc.tensor.transpose(pb[:, 0:P], bgf[:], ident[:])
-            nc.vector.tensor_copy(out=bgT[:], in_=pb[:, 0:8])
-            for h in range(2):
-                pbo = bank(1 + h)
-                nc.tensor.matmul(pbo[:], lhsT=ones[:], rhs=bopad[:, 512 * h : 512 * h + 512], start=True, stop=True)
-                nc.scalar.copy(out=bo_bc[:, 512 * h : 512 * h + 512], in_=pbo[:])
+        for item in LOADS:
+            load(*item)
 
-        r_raw = [raw.tile([P, 1024], BF16, name="rraw%d" % i) for i in range(8)]
-        x_raw = [raw.tile([P, 2, 1024], BF16, name="xraw%d" % j) for j in range(4)]
-        w_raw = {(w, g): raw.tile([P, 4, 1024], BF16, name="%sraw%d" % (w, g)) for w in ("wg", "wo") for g in range(2)}
+        bg_rows32 = const.tile([P, P], F32, name="bg_rows32")
+        nc.vector.tensor_copy(out=bg_rows32[:], in_=bg_rows[:])
+        bg_bank = bank()
+        nc.tensor.transpose(bg_bank[:, 0:P], bg_rows32[:], identity[:])
+        bg_col = const.tile([P, HEADS], F32, name="bg_col")
+        nc.vector.tensor_copy(out=bg_col[:], in_=bg_bank[:, 0:HEADS])
+        bo_all = const.tile([P, 1024], F32, name="bo_all")
+        for h in range(2):
+            cols = slice(512 * h, 512 * h + 512)
+            bo_bank = bank()
+            nc.tensor.matmul(bo_bank[:], lhsT=ones[:], rhs=bo_row[:, cols], start=True, stop=True)
+            nc.scalar.copy(out=bo_all[:, cols], in_=bo_bank[:])
 
-        def ld_r(i):
-            nc.sync.dma_start(out=r_raw[i][:], in_=rv[:, i, :])
-
-        def ld_x(j):
-            nc.sync.dma_start(out=x_raw[j][:], in_=xv[:, 2 * j : 2 * j + 2, :])
-
-        def ld_wg(g):
-            nc.sync.dma_start(
-                out=w_raw[("wg", g)][:].rearrange("p (u e) n -> p u (e n)", u=2),
-                in_=Wg[512 * g : 512 * g + 512, :].rearrange("(u p e) n -> p u (e n)", u=2, e=2),
-            )
-
-        def ld_wo(g, h):
-            nc.sync.dma_start(
-                out=w_raw[("wo", g)][:, :, 512 * h : 512 * h + 512],
-                in_=Wo[512 * g : 512 * g + 512, 512 * h : 512 * h + 512].rearrange("(t p) n -> p t n", p=P),
-            )
-
-        def silu_table():
-            nc.scalar.activation(out=warm[:], in_=epst[:], func=ACT.Silu)
-
-        def mx_tiles(nm, width):
+        def mx_operand(name):
             return (
-                mxp.tile([P, width], U32, name=nm + "q", align_bytes=64),
-                mxp.tile([P, width], U8, name=nm + "s", align_bytes=64),
+                packed.tile([P, 512], U32, name=name + "_codes", align_bytes=64),
+                packed.tile([P, 512], U8, name=name + "_scales", align_bytes=64),
             )
 
-        xq = {(g, b): mx_tiles("x%d%d" % (g, b), 512) for g in range(2) for b in range(2)}
-        wq = {(w, g, h): mx_tiles("%s%d%d" % (w, g, h), 512) for w in ("wg", "wo") for g in range(2) for h in range(2)}
-        hq = {(g, b): mx_tiles("h%d%d" % (g, b), 512) for g in range(2) for b in range(2)}
+        x_mx = {(g, b): mx_operand("x%d%d" % (g, b)) for g in range(2) for b in range(2)}
+        w_mx = {(w, g, h): mx_operand("%s%d%d" % (w, g, h)) for w in ("wg", "wo") for g in range(2) for h in range(2)}
+        h_mx = {(g, b): mx_operand("h%d%d" % (g, b)) for g in range(2) for b in range(2)}
 
-        def quantise(dst, src, lo=0, n=512):
+        def grouped_tile(tag, bufs):
+            return grouped.tile([P, 2048], BF16, name=tag, bufs=bufs, align_bytes=64)
+
+        def quantise(operand, source, first=0, words=512):
             nc.vector.quantize_mx(
-                out=dst[0][:, lo : lo + n].bitcast(FP8X4), scales=dst[1][:, lo : lo + n], in_=src[:, 4 * lo : 4 * lo + 4 * n]
+                out=operand[0][:, first : first + words].bitcast(FP8X4),
+                scales=operand[1][:, first : first + words],
+                in_=source[:, 4 * first : 4 * (first + words)],
             )
 
-        rstd = stat.tile([P, 64], F32, name="rstd")
-        nmr = stat.tile([P, 64], F32, name="nmr")
-        st = [stat.tile([P, 16, 6], F32, name="st%d" % j) for j in range(4)]
-        sm = [stat.tile([P, 16, 2], F32, name="sm%d" % j) for j in range(4)]
-        sd = [stat.tile([P, 16], F32, name="sd%d" % j) for j in range(4)]
-
-        def bn(i, short=()):
-            for h in range(8):
-                nc.vector.bn_stats(out=st[i // 2][:, 8 * (i % 2) + h, :], in_=r_raw[i][:, P * h : P * h + P])
-                if h % 2 == 0 and h // 2 < len(short):
-                    short[h // 2]()
-            for f in short[4:]:
-                f()
-
-        vv = {}
-
-        def weave(long_ops, short):
-            for k, f in enumerate(long_ops):
-                f()
-                if k < len(short):
-                    short[k]()
-            for f in short[len(long_ops) :]:
-                f()
-
-        def cmb(j):
-            d = stat.tile([P, 16], F32, name="d%d" % j)
-            d2 = stat.tile([P, 16], F32, name="dd%d" % j)
-            v = stat.tile([P, 16], F32, name="v%d" % j)
-            ve = stat.tile([P, 16], F32, name="ve%d" % j)
-
-            vv[j] = ve
-            return [
-                lambda: nc.vector.tensor_tensor(out=d[:], in0=st[j][:, :, 1], in1=st[j][:, :, 4], op=ALU.subtract),
-                lambda: nc.vector.tensor_reduce(
-                    out=sm[j][:], in_=st[j][:].rearrange("p n (a k) -> p n k a", a=2)[:, :, 1:3, :], axis=AX.X, op=ALU.add
-                ),
-                lambda: nc.vector.tensor_tensor(out=d2[:], in0=d[:], in1=d[:], op=ALU.mult),
-                lambda: nc.vector.scalar_tensor_tensor(
-                    out=v[:], in0=d2[:], scalar=32.0, in1=sm[j][:, :, 1], op0=ALU.mult, op1=ALU.add
-                ),
-                lambda: nc.vector.tensor_scalar(
-                    out=ve[:], in0=v[:], scalar1=1.0 / 128.0, scalar2=EPS, op0=ALU.mult, op1=ALU.add
-                ),
-            ]
-
-        def sq(j):
-            if j in POW:
-                nc.gpsimd.tensor_tensor(out=rstd[:, 16 * j : 16 * j + 16], in0=vv[j][:], in1=mhalf[:], op=ALU.pow)
-            else:
-                nc.scalar.activation(out=sd[j][:], in_=vv[j][:], func=ACT.Sqrt)
-
-        dealt = [0]
-
-        def drip(todo):
-            if dealt[0] < len(todo):
-                todo[dealt[0]]()
-                dealt[0] += 1
-
-        def flush(todo):
-            for f in todo[dealt[0] :]:
-                f()
-            dealt[0] = len(todo)
-
-        def fin(j):
-            cols = slice(16 * j, 16 * j + 16)
-            return ([] if j in POW else [lambda: nc.vector.reciprocal(out=rstd[:, cols], in_=sd[j][:])]) + [
-                lambda: nc.vector.scalar_tensor_tensor(
-                    out=nmr[:, cols], in0=sm[j][:, :, 0], scalar=-0.5, in1=rstd[:, cols], op0=ALU.mult, op1=ALU.mult
-                ),
-            ]
-
-        catn = {}
-
-        def nrm(i):
-            t = catp.tile([P, 1024], F32, name="catn")
-            for h in range(8):
-                c = 8 * i + h
-                nc.scalar.activation(
-                    out=t[:, P * h : P * h + P],
-                    in_=r_raw[i][:, P * h : P * h + P],
-                    func=ACT.Identity,
-                    bias=nmr[:, c : c + 1],
-                    scale=rstd[:, c : c + 1],
-                )
-            catn[i] = t
-
-        xin = {}
-
-        xts = {}
-
-        def xTp(i, k):
-            xw = x_raw[i // 2][:, i % 2, :].bitcast(F32)
-            xt = bank(k)
-            for w in range(4):
-                nc.tensor.transpose(xt[:, P * w : P * w + P], xw[:, P * w : P * w + P], ident[:])
-            xts[i] = xt
-
-        def xTs(i):
-            b, ii = i // 4, i % 4
+        def mx_group(acc, stationary, cols, moving):
             for g in range(2):
-                if (g, b) not in xin:
-                    xin[(g, b)] = grp.tile([P, 2048], BF16, name="xin", tag="xh", align_bytes=64)
-                nc.scalar.copy(
-                    out=xin[(g, b)][:].bitcast(F32)[:, 256 * ii : 256 * ii + 256].rearrange("p (r u) -> p r u", u=2),
-                    in_=xts[i][:, 256 * g : 256 * g + 256].rearrange("p (u r) -> p r u", u=2),
-                )
-
-        def xQ(g, b):
-            quantise(xq[(g, b)], xin[(g, b)])
-
-        win = {}
-
-        def rg(eng, w, g, h):
-            t = grp.tile([P, 2048], BF16, name="win", tag="win%d%d" % (g, h), bufs=1, align_bytes=64)
-            dst = t[:].rearrange("p (c i t) -> p c t i", i=4, t=4)
-            s = w_raw[(w, g)][:, :, 512 * h : 512 * h + 512].rearrange("p t (c i) -> p c t i", i=4)
-            if eng == "V":
-                nc.vector.tensor_copy(out=dst, in_=s)
-            elif eng == "S":
-                nc.scalar.copy(out=dst, in_=s)
-            else:
-                nc.gpsimd.tensor_scalar(
-                    out=t[:].rearrange("p (n t) -> p n t", t=4),
-                    in0=w_raw[(w, g)][:, :, 512 * h : 512 * h + 512].rearrange("p t n -> p n t"),
-                    scalar1=1.0,
-                    scalar2=0.0,
-                    op0=ALU.mult,
-                    op1=ALU.add,
-                )
-            win[(w, g, h)] = t
-
-        def wQ(w, g, h):
-            quantise(wq[(w, g, h)], win[(w, g, h)])
-
-        gate = {}
-
-        ps1 = {}
-
-        def s1p(b, c, k):
-            gr, t = c // 4, c % 4
-            ps = bank(k)
-            for g in range(2):
-                cq, cs = wq[("wg", g, gr)]
                 nc.tensor.matmul_mx(
-                    out=ps[:],
-                    lhsT=cq[:, P * t : P * t + P].bitcast(FP8X4),
-                    lhsT_scale=cs[:, P * t : P * t + P],
-                    rhs=xq[(g, b)][0][:].bitcast(FP8X4),
-                    rhs_scale=xq[(g, b)][1][:],
+                    out=acc[:],
+                    lhsT=stationary[g][0][:, cols].bitcast(FP8X4),
+                    lhsT_scale=stationary[g][1][:, cols],
+                    rhs=moving[g][0][:].bitcast(FP8X4),
+                    rhs_scale=moving[g][1][:],
                     start=(g == 0),
                     stop=(g == 1),
                 )
-            ps1[(b, c)] = ps
 
-        def s1a(b, c):
-            gr, t = c // 4, c % 4
-            if (b, gr) not in gate:
-                gate[(b, gr)] = gatep.tile([P, 4, 512], F32, name="gate%d%d" % (b, gr))
-            nc.scalar.activation(
-                out=gate[(b, gr)][:, t, :], in_=ps1[(b, c)][:], func=ACT.Silu, bias=bgT[:, c : c + 1], scale=1.0
+        def weave(long_steps, short_steps, places):
+            for k, step in enumerate(long_steps):
+                step()
+                for place, short in zip(places, short_steps):
+                    if place == k:
+                        short()
+
+        rstd = stat.tile([P, 64], F32, name="rstd")
+        shift = stat.tile([P, 64], F32, name="shift")
+        halves = [stat.tile([P, 2 * HEADS, 6], F32, name="halves%d" % j) for j in range(4)]
+        sums = [stat.tile([P, 2 * HEADS, 2], F32, name="sums%d" % j) for j in range(4)]
+        var_eps = [stat.tile([P, 2 * HEADS], F32, name="var_eps%d" % j) for j in range(4)]
+
+        def statistics(i, short_steps=()):
+            def head(c):
+                return lambda: nc.vector.bn_stats(
+                    out=halves[i // 2][:, HEADS * (i % 2) + c, :], in_=r_raw[i][:, P * c : P * c + P]
+                )
+
+            weave([head(c) for c in range(HEADS)], short_steps, (0, 1, 3, 5, 7))
+
+        def join(j):
+            diff = stat.tile([P, 2 * HEADS], F32, name="diff%d" % j)
+            square = stat.tile([P, 2 * HEADS], F32, name="square%d" % j)
+            m2 = stat.tile([P, 2 * HEADS], F32, name="m2%d" % j)
+            even_odd = halves[j][:].rearrange("p n (a k) -> p n k a", a=2)
+            return [
+                lambda: nc.vector.tensor_tensor(
+                    out=diff[:], in0=halves[j][:, :, 1], in1=halves[j][:, :, 4], op=ALU.subtract
+                ),
+                lambda: nc.vector.tensor_reduce(out=sums[j][:], in_=even_odd[:, :, 1:3, :], axis=AX.X, op=ALU.add),
+                lambda: nc.vector.tensor_tensor(out=square[:], in0=diff[:], in1=diff[:], op=ALU.mult),
+                lambda: nc.vector.scalar_tensor_tensor(
+                    out=m2[:], in0=square[:], scalar=32.0, in1=sums[j][:, :, 1], op0=ALU.mult, op1=ALU.add
+                ),
+                lambda: nc.vector.tensor_scalar(
+                    out=var_eps[j][:], in0=m2[:], scalar1=1.0 / P, scalar2=EPS, op0=ALU.mult, op1=ALU.add
+                ),
+            ]
+
+        def root(j):
+            cols = slice(16 * j, 16 * j + 16)
+            nc.gpsimd.tensor_tensor(out=rstd[:, cols], in0=var_eps[j][:], in1=minus_half[:], op=ALU.pow)
+
+        def finish(j):
+            cols = slice(16 * j, 16 * j + 16)
+            nc.vector.scalar_tensor_tensor(
+                out=shift[:, cols], in0=sums[j][:, :, 0], scalar=-0.5, in1=rstd[:, cols], op0=ALU.mult, op1=ALU.mult
             )
 
-        hin = {}
-        cts = {}
+        cat = {}
 
-        def ct(i, gr, k):
-            t_ = bank(k)
+        def normalise(i):
+            cat[i] = cat_pool.tile([P, 1024], F32, name="cat")
+            for c in range(HEADS):
+                col = HEADS * i + c
+                nc.scalar.activation(
+                    out=cat[i][:, P * c : P * c + P],
+                    in_=r_raw[i][:, P * c : P * c + P],
+                    func=ACT.Identity,
+                    bias=shift[:, col : col + 1],
+                    scale=rstd[:, col : col + 1],
+                )
+
+        x_bank = {}
+        x_grouped = {}
+
+        def x_transpose(i):
+            words = x_raw[i // 2][:, i % 2, :].bitcast(F32)
+            x_bank[i] = bank()
+            for gu in range(4):
+                nc.tensor.transpose(x_bank[i][:, P * gu : P * gu + P], words[:, P * gu : P * gu + P], identity[:])
+
+        def x_copy(i):
+            b, place = i // 4, i % 4
+            for g in range(2):
+                if place == 0:
+                    x_grouped[(g, b)] = grouped_tile("x_or_h", 4)
+                nc.scalar.copy(
+                    out=x_grouped[(g, b)][:].bitcast(F32)[:, 256 * place : 256 * place + 256].rearrange(
+                        "p (r u) -> p r u", u=2
+                    ),
+                    in_=x_bank[i][:, 256 * g : 256 * g + 256].rearrange("p (u r) -> p r u", u=2),
+                )
+
+        def x_quantise(b):
+            for g in range(2):
+                quantise(x_mx[(g, b)], x_grouped[(g, b)])
+
+        w_grouped = {}
+
+        def regroup(copy, w, g, h):
+            w_grouped[(w, g, h)] = grouped_tile("w%d%d" % (g, h), 1)
+            copy(
+                out=w_grouped[(w, g, h)][:].rearrange("p (c i t) -> p c t i", i=4, t=4),
+                in_=w_raw[(w, g)][:, :, 512 * h : 512 * h + 512].rearrange("p t (c i) -> p c t i", i=4),
+            )
+
+        def w_quantise(w, g, h):
+            quantise(w_mx[(w, g, h)], w_grouped[(w, g, h)])
+
+        on_scalar = nc.scalar.copy
+        on_vector = nc.vector.tensor_copy
+
+        gate_bank = {}
+        gate = {}
+
+        def gate_matmuls(b, c):
+            gate_bank[(b, c)] = bank()
+            mx_group(
+                gate_bank[(b, c)],
+                [w_mx[("wg", g, c // 4)] for g in range(2)],
+                slice(P * (c % 4), P * (c % 4) + P),
+                [x_mx[(g, b)] for g in range(2)],
+            )
+
+        def gate_silu(b, c):
+            if c % 4 == 0:
+                gate[(b, c // 4)] = gate_pool.tile([P, 4, 512], F32, name="gate%d%d" % (b, c // 4))
+            nc.scalar.activation(
+                out=gate[(b, c // 4)][:, c % 4, :],
+                in_=gate_bank[(b, c)][:],
+                func=ACT.Silu,
+                bias=bg_col[:, c : c + 1],
+                scale=1.0,
+            )
+
+        cat_bank = {}
+        h_grouped = {}
+
+        def cat_transpose(i, g):
+            cat_bank[(i, g)] = bank()
             for t in range(4):
-                c0 = 512 * gr + P * t
-                nc.tensor.transpose(t_[:, P * t : P * t + P], catn[i][:, c0 : c0 + P], ident[:])
-            cts[(i, gr)] = t_
+                c = 4 * g + t
+                nc.tensor.transpose(cat_bank[(i, g)][:, P * t : P * t + P], cat[i][:, P * c : P * c + P], identity[:])
 
-        def mul(i, gr):
-            b, ii = i // 4, i % 4
-            if (gr, b) not in hin:
-                hin[(gr, b)] = grp.tile([P, 2048], BF16, name="hin", tag="xh", align_bytes=64)
+        def multiply(i, g):
+            b, place = i // 4, i % 4
+            if place == 0:
+                h_grouped[(g, b)] = grouped_tile("x_or_h", 4)
             nc.vector.tensor_tensor(
-                out=hin[(gr, b)][:, 512 * ii : 512 * ii + 512].rearrange("p (r t) -> p r t", t=4),
-                in0=gate[(b, gr)][:, :, P * ii : P * ii + P].rearrange("p t r -> p r t"),
-                in1=cts[(i, gr)][:].rearrange("p (t r) -> p r t", t=4),
+                out=h_grouped[(g, b)][:, 512 * place : 512 * place + 512].rearrange("p (r t) -> p r t", t=4),
+                in0=gate[(b, g)][:, :, P * place : P * place + P].rearrange("p t r -> p r t"),
+                in1=cat_bank[(i, g)][:].rearrange("p (t r) -> p r t", t=4),
                 op=ALU.mult,
             )
 
-        def hQ(gr, b, lo=0, n=512):
-            quantise(hq[(gr, b)], hin[(gr, b)], lo, n)
-
-        ots = {}
-
-        ps2 = {}
-
-        def s2p(i, h, k):
-            b, ii = i // 4, i % 4
-            ps = bank(k)
+        def h_quantise(b, half):
             for g in range(2):
-                nc.tensor.matmul_mx(
-                    out=ps[:],
-                    lhsT=hq[(g, b)][0][:, P * ii : P * ii + P].bitcast(FP8X4),
-                    lhsT_scale=hq[(g, b)][1][:, P * ii : P * ii + P],
-                    rhs=wq[("wo", g, h)][0][:].bitcast(FP8X4),
-                    rhs_scale=wq[("wo", g, h)][1][:],
-                    start=(g == 0),
-                    stop=(g == 1),
+                quantise(h_mx[(g, b)], h_grouped[(g, b)], 256 * half, 256)
+
+        out_bank = {}
+        out_tile = {}
+
+        def out_matmuls(i, h):
+            out_bank[(i, h)] = bank()
+            place = i % 4
+            mx_group(
+                out_bank[(i, h)],
+                [h_mx[(g, i // 4)] for g in range(2)],
+                slice(P * place, P * place + P),
+                [w_mx[("wo", g, h)] for g in range(2)],
+            )
+
+        def out_bias(i, h):
+            if h == 0:
+                out_tile[i] = out_pool.tile([P, 1024], F32, name="out_tile")
+            cols = slice(512 * h, 512 * h + 512)
+            nc.vector.tensor_tensor(out=out_tile[i][:, cols], in0=out_bank[(i, h)][:], in1=bo_all[:, cols], op=ALU.add)
+            if h == 1:
+                nc.sync.dma_start(out=out_tiles[:, i, :], in_=out_tile[i][:])
+
+
+        statistics(0)
+        statistics(1)
+        statistics(2, join(0))
+        root(0)
+        regroup(on_scalar, "wg", 0, 0)
+        regroup(on_scalar, "wg", 0, 1)
+        w_quantise("wg", 0, 0)
+        statistics(3)
+        statistics(4, join(1))
+        root(1)
+        finish(0)
+        for i in range(4):
+            x_transpose(i)
+        for i in range(4):
+            x_copy(i)
+        regroup(on_scalar, "wo", 0, 0)
+        normalise(0)
+        normalise(1)
+        x_quantise(0)
+        regroup(on_vector, "wg", 1, 0)
+        w_quantise("wg", 0, 1)
+        statistics(5)
+        w_quantise("wo", 0, 0)
+        w_quantise("wg", 1, 0)
+        finish(1)
+        regroup(on_vector, "wg", 1, 1)
+        statistics(6, join(2))
+        root(2)
+        for i in range(4, 8):
+            x_transpose(i)
+        for i in range(4, 8):
+            x_copy(i)
+        normalise(2)
+        normalise(3)
+        w_quantise("wg", 1, 1)
+        statistics(7)
+        regroup(on_vector, "wo", 1, 1)
+        x_quantise(1)
+        finish(2)
+
+        for b in range(2):
+            tiles = range(4 * b, 4 * b + 4)
+            for c in range(HEADS):
+                gate_matmuls(b, c)
+            for c in range(HEADS):
+                gate_silu(b, c)
+            if b == 0:
+                regroup(on_scalar, "wo", 1, 0)
+                regroup(on_scalar, "wo", 0, 1)
+            else:
+                for i in range(4):
+                    for h in range(2):
+                        out_matmuls(i, h)
+                for i in range(4):
+                    for h in range(2):
+                        out_bias(i, h)
+                    if i == 0:
+                        finish(3)
+                for i in tiles:
+                    normalise(i)
+            for i in tiles:
+                for g in range(2):
+                    cat_transpose(i, g)
+            first, second, third, fourth = tiles
+            if b == 0:
+                weave(
+                    [
+                        lambda: w_quantise("wo", 1, 1),
+                        lambda: multiply(first, 0),
+                        lambda: multiply(first, 1),
+                        lambda: multiply(second, 0),
+                        lambda: multiply(second, 1),
+                    ],
+                    join(3),
+                    range(5),
                 )
-            ps2[(i, h)] = ps
+                root(3)
+            else:
+                for i in (first, second):
+                    for g in range(2):
+                        multiply(i, g)
+            h_quantise(b, 0)
+            for g in range(2):
+                multiply(third, g)
+            if b == 0:
+                w_quantise("wo", 1, 0)
+            for g in range(2):
+                multiply(fourth, g)
+            if b == 0:
+                w_quantise("wo", 0, 1)
+            h_quantise(b, 1)
 
-        def oslice(i, h):
-            if i not in ots:
-                ots[i] = outp.tile([P, 1024], F32, name="ot")
-            return ots[i][:, 512 * h : 512 * h + 512]
-
-        def s2e(i, h):
-            nc.vector.tensor_tensor(out=oslice(i, h), in0=ps2[(i, h)][:], in1=bo_bc[:, 512 * h : 512 * h + 512], op=ALU.add)
-
-        def s2c(i, h):
-            nc.scalar.copy(out=oslice(i, h), in_=ps2[(i, h)][:])
-
-        def s2g(i, h):
-            nc.gpsimd.tensor_tensor(out=oslice(i, h), in0=oslice(i, h), in1=bo_bc[:, 512 * h : 512 * h + 512], op=ALU.add)
-
-        def st_(i):
-            nc.sync.dma_start(out=ov[:, i, :], in_=ots[i][:])
-
-        HQW = 256
-        POW = (3,)
-        consts()
-        bias()
-        ld_wg(0)
-        ld_r(0)
-        ld_r(1)
-        ld_x(3)
-        ld_r(2)
-        ld_x(1)
-        ld_r(3)
-        ld_x(0)
-        ld_r(4)
-        rg("S", "wg", 0, 1)
-        ld_wg(1)
-        bn(0)
-        ld_x(2)
-        ld_r(5)
-        bn(1)
-        rg("S", "wg", 0, 0)
-        xTp(7, 0)
-        ld_wo(1, 0)
-        ld_wo(1, 1)
-        bn(2, cmb(0))
-        xTp(2, 1)
-        ld_r(6)
-        xTs(7)
-        xTp(3, 2)
-        xTp(6, 3)
-        ld_wo(0, 1)
-        xTs(2)
-        wQ("wg", 0, 0)
-        sq(0)
-        xTs(6)
-        xTp(0, 4)
-        bn(3, fin(0))
-        ld_r(7)
-        xTs(3)
-        xTp(1, 5)
-        ld_wo(0, 0)
-        xTs(0)
-        xTs(1)
-        bn(4, cmb(1))
-        nrm(1)
-        nrm(0)
-        rg("V", "wg", 1, 0)
-        xTp(4, 6)
-        xTp(5, 7)
-        xQ(0, 0)
-        sq(1)
-        xTs(4)
-        wQ("wg", 1, 0)
-        xTs(5)
-        xQ(1, 0)
-        rg("S", "wo", 1, 0)
-        bn(5, fin(1))
-        s1p(0, 2, 0)
-        s1p(0, 0, 1)
-        rg("V", "wg", 1, 1)
-        s1p(0, 1, 3)
-        nrm(3)
-        s1p(0, 3, 2)
-        bn(6, cmb(2))
-        nrm(2)
-        wQ("wg", 1, 1)
-        sq(2)
-        xQ(1, 1)
-        s1a(0, 1)
-        ct(2, 0, 4)
-        wQ("wg", 0, 1)
-        ct(1, 0, 5)
-        xQ(0, 1)
-        s1p(0, 6, 6)
-        bn(7, fin(2))
-        s1a(0, 2)
-        s1p(0, 7, 7)
-        s1a(0, 3)
-        s1p(0, 5, 3)
-        s1a(0, 0)
-        ct(3, 1, 0)
-        c3 = cmb(3)
-        wQ("wo", 1, 0)
-        drip(c3)
-        ct(3, 0, 2)
-        s1a(0, 5)
-        s1p(0, 4, 1)
-        mul(1, 0)
-        drip(c3)
-        s1a(0, 6)
-        mul(3, 0)
-        drip(c3)
-        s1p(1, 2, 3)
-        s1a(0, 7)
-        rg("V", "wo", 1, 1)
-        drip(c3)
-        s1p(1, 3, 5)
-        s1a(0, 4)
-        ct(0, 1, 6)
-        rg("S", "wo", 0, 0)
-        ct(2, 1, 2)
-        mul(2, 0)
-        drip(c3)
-        ct(1, 1, 7)
-        flush(c3)
-        sq(3)
-        mul(0, 1)
-        s1p(1, 1, 1)
-        mul(3, 1)
-        ct(0, 0, 4)
-        mul(2, 1)
-        s1p(1, 5, 6)
-        rg("S", "wo", 0, 1)
-        hQ(0, 0, HQW * 1, HQW)
-        s1p(1, 4, 0)
-        mul(0, 0)
-        s1p(1, 0, 2)
-        hQ(1, 0, HQW * 1, HQW)
-        wQ("wo", 0, 0)
-        s1p(1, 7, 4)
-        wQ("wo", 1, 1)
-        s1a(1, 3)
-        wQ("wo", 0, 1)
-        s1a(1, 2)
-        s2p(3, 0, 5)
-        mul(1, 1)
-        s1a(1, 5)
-        s2p(3, 1, 3)
-        weave([], fin(3))
-        hQ(0, 0, HQW * 0, HQW)
-        s1a(1, 1)
-        hQ(1, 0, HQW * 0, HQW)
-        s2p(2, 0, 7)
-        s2e(3, 0)
-        nrm(7)
-        s2p(0, 1, 6)
-        s2e(2, 0)
-        s2p(0, 0, 1)
-        nrm(4)
-        s2e(0, 1)
-        s1p(1, 6, 5)
-        s2e(0, 0)
-        s2p(2, 1, 7)
-        s2e(3, 1)
-        s1a(1, 0)
-        s2p(1, 0, 6)
-        s2e(2, 1)
-        nrm(6)
-        ct(4, 0, 1)
-        s2e(1, 0)
-        ct(7, 0, 3)
-        st_(2)
-        ct(4, 1, 2)
-        st_(3)
-        mul(4, 0)
-        st_(0)
-        s2p(1, 1, 7)
-        s1a(1, 4)
-        mul(7, 0)
-        ct(6, 0, 6)
-        s1a(1, 6)
-        s2e(1, 1)
-        ct(6, 1, 1)
-        s1a(1, 7)
-        ct(7, 1, 0)
-        mul(6, 0)
-        nrm(5)
-        st_(1)
-        mul(7, 1)
-        mul(6, 1)
-        hQ(0, 1, HQW * 1, HQW)
-        ct(5, 0, 3)
-        hQ(1, 1, HQW * 1, HQW)
-        ct(5, 1, 5)
-        mul(4, 1)
-        s2p(7, 1, 7)
-        mul(5, 0)
-        mul(5, 1)
-        s2p(6, 1, 4)
-        s2e(7, 1)
-        s2p(7, 0, 6)
-        hQ(0, 1, HQW * 0, HQW)
-        s2p(6, 0, 0)
-        hQ(1, 1, HQW * 0, HQW)
-        s2e(7, 0)
-        s2p(5, 0, 1)
-        s2e(6, 1)
-        st_(7)
-        s2p(5, 1, 2)
-        s2e(6, 0)
-        s2p(4, 0, 3)
-        s2e(5, 0)
-        st_(6)
-        s2p(4, 1, 5)
-        s2e(5, 1)
-        s2e(4, 0)
-        st_(5)
-        s2e(4, 1)
-        st_(4)
+        for i in range(4, 8):
+            for h in range(2):
+                out_matmuls(i, h)
+        for i in range(4, 8):
+            for h in range(2):
+                out_bias(i, h)

@@ -19,11 +19,6 @@ HEADS = 8
 EPS = 1e-5
 BANKS = 8
 
-LOADS = (
-    ("r", 0), ("wg", 0, 0), ("r", 1), ("wg", 0, 1), ("r", 2), ("x", 0), ("x", 1), ("r", 3), ("wo", 0, 0), ("r", 4),
-    ("wg", 1, 0), ("x", 2), ("r", 5), ("x", 3), ("wg", 1, 1), ("wo", 1, 1), ("r", 6), ("r", 7), ("wo", 1, 0), ("wo", 0, 1),
-)
-
 
 def tile_gatedmultiscaleretentionlayer_pa_kernel(tc, x, ret_cat, Wg, bg, Wo, bo, out):
     nc = tc.nc
@@ -60,10 +55,12 @@ def tile_gatedmultiscaleretentionlayer_pa_kernel(tc, x, ret_cat, Wg, bg, Wo, bo,
         nc.vector.memset(ones[:], 1.0)
         minus_half = const.tile([P, 2 * HEADS], F32, name="minus_half")
         nc.vector.memset(minus_half[:], -0.5)
+        ones_col = const.tile([P, 1], F32, name="ones_col")
+        nc.vector.memset(ones_col[:], 1.0)
         nc.scalar.dma_start(out=bg_rows[0:HEADS, :], in_=bg.rearrange("(c p) -> c p", p=P))
         nc.scalar.dma_start(out=bo_row[0:1, :], in_=bo.rearrange("(o d) -> o d", o=1))
         scratch = const.tile([P, 1], F32, name="scratch")
-        nc.scalar.activation(out=scratch[:], in_=minus_half[:, 0:1], func=ACT.Silu)
+        nc.scalar.activation(out=scratch[:], in_=ones_col[:], func=ACT.Sqrt)
 
         r_raw = [raw.tile([P, 1024], BF16, name="r_raw%d" % i) for i in range(8)]
         x_raw = [raw.tile([P, 2, 1024], BF16, name="x_raw%d" % j) for j in range(4)]
@@ -87,9 +84,6 @@ def tile_gatedmultiscaleretentionlayer_pa_kernel(tc, x, ret_cat, Wg, bg, Wo, bo,
                     out=w_raw[("wo", a)][:, :, cols],
                     in_=Wo[512 * a : 512 * a + 512, cols].rearrange("(t p) n -> p t n", p=P),
                 )
-
-        for item in LOADS:
-            load(*item)
 
         bg_rows32 = const.tile([P, P], F32, name="bg_rows32")
         nc.vector.tensor_copy(out=bg_rows32[:], in_=bg_rows[:])
@@ -155,7 +149,7 @@ def tile_gatedmultiscaleretentionlayer_pa_kernel(tc, x, ret_cat, Wg, bg, Wo, bo,
                     out=halves[i // 2][:, HEADS * (i % 2) + c, :], in_=r_raw[i][:, P * c : P * c + P]
                 )
 
-            weave([head(c) for c in range(HEADS)], short_steps, (0, 1, 3, 5, 7))
+            weave([head(c) for c in range(HEADS)], short_steps, (0, 1, 3, 5, 7) if len(short_steps) > 2 else (2, 5))
 
         def join(j):
             diff = stat.tile([P, 2 * HEADS], F32, name="diff%d" % j)
@@ -176,15 +170,24 @@ def tile_gatedmultiscaleretentionlayer_pa_kernel(tc, x, ret_cat, Wg, bg, Wo, bo,
                 ),
             ]
 
+        std = [stat.tile([P, 2 * HEADS], F32, name="std%d" % j) for j in range(3)]
+
         def root(j):
-            cols = slice(16 * j, 16 * j + 16)
-            nc.gpsimd.tensor_tensor(out=rstd[:, cols], in0=var_eps[j][:], in1=minus_half[:], op=ALU.pow)
+            if j < 3:
+                nc.scalar.activation(out=std[j][:], in_=var_eps[j][:], func=ACT.Sqrt)
+            else:
+                nc.gpsimd.tensor_tensor(out=rstd[:, 48:64], in0=var_eps[j][:], in1=minus_half[:], op=ALU.pow)
 
         def finish(j):
             cols = slice(16 * j, 16 * j + 16)
-            nc.vector.scalar_tensor_tensor(
-                out=shift[:, cols], in0=sums[j][:, :, 0], scalar=-0.5, in1=rstd[:, cols], op0=ALU.mult, op1=ALU.mult
-            )
+            steps = [
+                lambda: nc.vector.scalar_tensor_tensor(
+                    out=shift[:, cols], in0=sums[j][:, :, 0], scalar=-0.5, in1=rstd[:, cols], op0=ALU.mult, op1=ALU.mult
+                )
+            ]
+            if j < 3:
+                steps = [lambda: nc.vector.reciprocal(out=rstd[:, cols], in_=std[j][:])] + steps
+            return steps
 
         cat = {}
 
@@ -308,102 +311,184 @@ def tile_gatedmultiscaleretentionlayer_pa_kernel(tc, x, ret_cat, Wg, bg, Wo, bo,
             if h == 1:
                 nc.sync.dma_start(out=out_tiles[:, i, :], in_=out_tile[i][:])
 
-
+        load("r", 0)
+        load("wg", 0, 0)
+        load("r", 1)
+        load("wg", 0, 1)
+        load("r", 2)
+        load("x", 0)
+        load("x", 1)
+        load("r", 3)
+        load("wo", 0, 0)
         statistics(0)
-        statistics(1)
-        statistics(2, join(0))
-        root(0)
+        load("r", 4)
         regroup(on_scalar, "wg", 0, 0)
+        load("wg", 1, 0)
+        statistics(1)
+        load("x", 2)
+        load("r", 5)
         regroup(on_scalar, "wg", 0, 1)
+        statistics(2, join(0))
+        load("x", 3)
+        x_transpose(0)
+        load("wg", 1, 1)
         w_quantise("wg", 0, 0)
-        statistics(3)
-        statistics(4, join(1))
-        root(1)
-        finish(0)
-        for i in range(4):
-            x_transpose(i)
-        for i in range(4):
-            x_copy(i)
+        x_transpose(1)
+        root(0)
+        x_copy(0)
+        x_transpose(2)
+        load("wo", 1, 1)
+        x_copy(1)
+        x_transpose(3)
+        statistics(3, finish(0))
+        load("r", 6)
+        x_copy(2)
+        x_copy(3)
+        load("r", 7)
         regroup(on_scalar, "wo", 0, 0)
-        normalise(0)
-        normalise(1)
+        statistics(4, join(1))
+        load("wo", 1, 0)
+        load("wo", 0, 1)
         x_quantise(0)
+        normalise(0)
+        x_transpose(4)
         regroup(on_vector, "wg", 1, 0)
+        x_transpose(5)
+        root(1)
+        normalise(1)
         w_quantise("wg", 0, 1)
-        statistics(5)
+        x_transpose(6)
+        statistics(5, finish(1))
+        x_copy(4)
+        x_transpose(7)
+        x_copy(5)
+        x_copy(6)
         w_quantise("wo", 0, 0)
+        x_copy(7)
         w_quantise("wg", 1, 0)
-        finish(1)
-        regroup(on_vector, "wg", 1, 1)
-        statistics(6, join(2))
-        root(2)
-        for i in range(4, 8):
-            x_transpose(i)
-        for i in range(4, 8):
-            x_copy(i)
         normalise(2)
+        statistics(6, join(2))
+        gate_matmuls(0, 0)
         normalise(3)
+        gate_matmuls(0, 1)
+        regroup(on_vector, "wg", 1, 1)
+        gate_matmuls(0, 2)
+        gate_matmuls(0, 3)
+        root(2)
+        gate_silu(0, 0)
         w_quantise("wg", 1, 1)
-        statistics(7)
-        regroup(on_vector, "wo", 1, 1)
+        statistics(7, finish(2))
+        gate_matmuls(0, 4)
+        gate_silu(0, 1)
+        gate_matmuls(0, 5)
         x_quantise(1)
-        finish(2)
-
-        for b in range(2):
-            tiles = range(4 * b, 4 * b + 4)
-            for c in range(HEADS):
-                gate_matmuls(b, c)
-            for c in range(HEADS):
-                gate_silu(b, c)
-            if b == 0:
-                regroup(on_scalar, "wo", 1, 0)
-                regroup(on_scalar, "wo", 0, 1)
-            else:
-                for i in range(4):
-                    for h in range(2):
-                        out_matmuls(i, h)
-                for i in range(4):
-                    for h in range(2):
-                        out_bias(i, h)
-                    if i == 0:
-                        finish(3)
-                for i in tiles:
-                    normalise(i)
-            for i in tiles:
-                for g in range(2):
-                    cat_transpose(i, g)
-            first, second, third, fourth = tiles
-            if b == 0:
-                weave(
-                    [
-                        lambda: w_quantise("wo", 1, 1),
-                        lambda: multiply(first, 0),
-                        lambda: multiply(first, 1),
-                        lambda: multiply(second, 0),
-                        lambda: multiply(second, 1),
-                    ],
-                    join(3),
-                    range(5),
-                )
-                root(3)
-            else:
-                for i in (first, second):
-                    for g in range(2):
-                        multiply(i, g)
-            h_quantise(b, 0)
-            for g in range(2):
-                multiply(third, g)
-            if b == 0:
-                w_quantise("wo", 1, 0)
-            for g in range(2):
-                multiply(fourth, g)
-            if b == 0:
-                w_quantise("wo", 0, 1)
-            h_quantise(b, 1)
-
-        for i in range(4, 8):
-            for h in range(2):
-                out_matmuls(i, h)
-        for i in range(4, 8):
-            for h in range(2):
-                out_bias(i, h)
+        gate_matmuls(0, 6)
+        gate_silu(0, 2)
+        gate_matmuls(0, 7)
+        gate_silu(0, 3)
+        regroup(on_vector, "wo", 1, 1)
+        cat_transpose(0, 0)
+        gate_silu(0, 4)
+        cat_transpose(0, 1)
+        gate_silu(0, 5)
+        last_join = join(3)
+        cat_transpose(1, 0)
+        gate_silu(0, 6)
+        w_quantise("wo", 1, 1)
+        last_join[0]()
+        cat_transpose(1, 1)
+        gate_silu(0, 7)
+        multiply(0, 0)
+        last_join[1]()
+        cat_transpose(2, 0)
+        cat_transpose(2, 1)
+        regroup(on_scalar, "wo", 1, 0)
+        multiply(0, 1)
+        last_join[2]()
+        cat_transpose(3, 0)
+        cat_transpose(3, 1)
+        multiply(1, 0)
+        last_join[3]()
+        gate_matmuls(1, 0)
+        multiply(1, 1)
+        last_join[4]()
+        gate_matmuls(1, 1)
+        root(3)
+        h_quantise(0, 0)
+        regroup(on_scalar, "wo", 0, 1)
+        gate_matmuls(1, 2)
+        multiply(2, 0)
+        gate_matmuls(1, 3)
+        multiply(2, 1)
+        gate_matmuls(1, 4)
+        w_quantise("wo", 1, 0)
+        gate_matmuls(1, 5)
+        gate_silu(1, 0)
+        multiply(3, 0)
+        gate_silu(1, 1)
+        multiply(3, 1)
+        gate_matmuls(1, 6)
+        gate_silu(1, 2)
+        w_quantise("wo", 0, 1)
+        gate_matmuls(1, 7)
+        gate_silu(1, 3)
+        h_quantise(0, 1)
+        out_matmuls(0, 0)
+        gate_silu(1, 4)
+        out_matmuls(0, 1)
+        gate_silu(1, 5)
+        out_bias(0, 0)
+        out_matmuls(1, 0)
+        gate_silu(1, 6)
+        out_bias(0, 1)
+        out_matmuls(1, 1)
+        gate_silu(1, 7)
+        finish(3)[0]()
+        out_bias(1, 0)
+        out_matmuls(2, 0)
+        normalise(4)
+        out_bias(1, 1)
+        out_matmuls(2, 1)
+        out_bias(2, 0)
+        out_matmuls(3, 0)
+        out_bias(2, 1)
+        out_matmuls(3, 1)
+        normalise(5)
+        out_bias(3, 0)
+        cat_transpose(4, 0)
+        out_bias(3, 1)
+        cat_transpose(4, 1)
+        normalise(6)
+        multiply(4, 0)
+        cat_transpose(5, 0)
+        cat_transpose(5, 1)
+        multiply(4, 1)
+        normalise(7)
+        multiply(5, 0)
+        cat_transpose(6, 0)
+        multiply(5, 1)
+        cat_transpose(6, 1)
+        h_quantise(1, 0)
+        cat_transpose(7, 0)
+        multiply(6, 0)
+        cat_transpose(7, 1)
+        multiply(6, 1)
+        out_matmuls(4, 0)
+        multiply(7, 0)
+        out_matmuls(4, 1)
+        multiply(7, 1)
+        out_matmuls(5, 0)
+        h_quantise(1, 1)
+        out_matmuls(5, 1)
+        out_bias(4, 0)
+        out_matmuls(6, 0)
+        out_bias(4, 1)
+        out_matmuls(6, 1)
+        out_bias(5, 0)
+        out_matmuls(7, 0)
+        out_bias(5, 1)
+        out_matmuls(7, 1)
+        out_bias(6, 0)
+        out_bias(6, 1)
+        out_bias(7, 0)
+        out_bias(7, 1)

@@ -308,8 +308,7 @@ def tile_gatedmultiscaleretentionlayer_pa_kernel(tc, x, ret_cat, Wg, bg, Wo, bo,
                 out_tile[i] = out_pool.tile([P, 1024], F32, name="out_tile")
             cols = slice(512 * h, 512 * h + 512)
             nc.vector.tensor_tensor(out=out_tile[i][:, cols], in0=out_bank[(i, h)][:], in1=bo_all[:, cols], op=ALU.add)
-            if h == 1:
-                nc.sync.dma_start(out=out_tiles[:, i, :], in_=out_tile[i][:])
+            nc.sync.dma_start(out=out_tiles[:, i, cols], in_=out_tile[i][:, cols])
 
         load("r", 0)
         load("wg", 0, 0)
@@ -411,9 +410,7 @@ def tile_gatedmultiscaleretentionlayer_pa_kernel(tc, x, ret_cat, Wg, bg, Wo, bo,
         last_join[3]()
         gate_matmuls(1, 0)
         multiply(1, 1)
-        last_join[4]()
         gate_matmuls(1, 1)
-        root(3)
         h_quantise(0, 0)
         regroup(on_scalar, "wo", 0, 1)
         gate_matmuls(1, 2)
@@ -437,13 +434,14 @@ def tile_gatedmultiscaleretentionlayer_pa_kernel(tc, x, ret_cat, Wg, bg, Wo, bo,
         gate_silu(1, 4)
         out_matmuls(0, 1)
         gate_silu(1, 5)
+        last_join[4]()
+        root(3)
         out_bias(0, 0)
         out_matmuls(1, 0)
         gate_silu(1, 6)
         out_bias(0, 1)
         out_matmuls(1, 1)
         gate_silu(1, 7)
-        finish(3)[0]()
         out_bias(1, 0)
         out_matmuls(2, 0)
         normalise(4)
@@ -455,6 +453,7 @@ def tile_gatedmultiscaleretentionlayer_pa_kernel(tc, x, ret_cat, Wg, bg, Wo, bo,
         out_matmuls(3, 1)
         normalise(5)
         out_bias(3, 0)
+        finish(3)[0]()
         cat_transpose(4, 0)
         out_bias(3, 1)
         cat_transpose(4, 1)

@@ -280,9 +280,9 @@ def tile_gatedmultiscaleretentionlayer_pa_kernel(tc, x, ret_cat, Wg, bg, Wo, bo,
             if place == 0:
                 h_grouped[(g, b)] = grouped_tile("x_or_h", 4)
             nc.vector.tensor_tensor(
-                out=h_grouped[(g, b)][:, 512 * place : 512 * place + 512].rearrange("p (r t) -> p r t", t=4),
-                in0=gate[(b, g)][:, :, P * place : P * place + P].rearrange("p t r -> p r t"),
-                in1=cat_bank[(i, g)][:].rearrange("p (t r) -> p r t", t=4),
+                out=h_grouped[(g, b)][:, 512 * place : 512 * place + 512].rearrange("p (c i t) -> p c t i", i=4, t=4),
+                in0=gate[(b, g)][:, :, P * place : P * place + P].rearrange("p t (c i) -> p c t i", i=4),
+                in1=cat_bank[(i, g)][:].rearrange("p (t c i) -> p c t i", t=4, i=4),
                 op=ALU.mult,
             )
 

@@ -139,34 +139,25 @@ def tile_gatedmultiscaleretentionlayer_pa_kernel(tc, x, ret_cat, Wg, bg, Wo, bo,
 
         rstd = stat.tile([P, 64], F32, name="rstd")
         shift = stat.tile([P, 64], F32, name="shift")
-        halves = [stat.tile([P, 2 * HEADS, 6], F32, name="halves%d" % j) for j in range(4)]
-        sums = [stat.tile([P, 2 * HEADS, 2], F32, name="sums%d" % j) for j in range(4)]
+        moments = [stat.tile([P, HEADS, 6], F32, name="moments%d" % j) for j in range(4)]
         var_eps = [stat.tile([P, 2 * HEADS], F32, name="var_eps%d" % j) for j in range(4)]
 
+        def by_head(j, k):
+            return moments[j][:].rearrange("p n (a k) -> p (n a) k", a=2)[:, :, k]
+
         def statistics(i, short_steps=()):
-            def head(c):
+            def two_heads(n):
                 return lambda: nc.vector.bn_stats(
-                    out=halves[i // 2][:, HEADS * (i % 2) + c, :], in_=r_raw[i][:, P * c : P * c + P]
+                    out=moments[i // 2][:, 4 * (i % 2) + n, :],
+                    in_=r_raw[i][:, 2 * P * n : 2 * P * n + 2 * P].rearrange("p (a k) -> p k a", a=2),
                 )
 
-            weave([head(c) for c in range(HEADS)], short_steps, (0, 1, 3, 5, 7) if len(short_steps) > 2 else (2, 5))
+            weave([two_heads(n) for n in range(4)], short_steps, (0, 2))
 
         def join(j):
-            diff = stat.tile([P, 2 * HEADS], F32, name="diff%d" % j)
-            square = stat.tile([P, 2 * HEADS], F32, name="square%d" % j)
-            m2 = stat.tile([P, 2 * HEADS], F32, name="m2%d" % j)
-            even_odd = halves[j][:].rearrange("p n (a k) -> p n k a", a=2)
             return [
-                lambda: nc.vector.tensor_tensor(
-                    out=diff[:], in0=halves[j][:, :, 1], in1=halves[j][:, :, 4], op=ALU.subtract
-                ),
-                lambda: nc.vector.tensor_reduce(out=sums[j][:], in_=even_odd[:, :, 1:3, :], axis=AX.X, op=ALU.add),
-                lambda: nc.vector.tensor_tensor(out=square[:], in0=diff[:], in1=diff[:], op=ALU.mult),
-                lambda: nc.vector.scalar_tensor_tensor(
-                    out=m2[:], in0=square[:], scalar=32.0, in1=sums[j][:, :, 1], op0=ALU.mult, op1=ALU.add
-                ),
                 lambda: nc.vector.tensor_scalar(
-                    out=var_eps[j][:], in0=m2[:], scalar1=1.0 / P, scalar2=EPS, op0=ALU.mult, op1=ALU.add
+                    out=var_eps[j][:], in0=by_head(j, 2), scalar1=1.0 / P, scalar2=EPS, op0=ALU.mult, op1=ALU.add
                 ),
             ]
 
@@ -182,7 +173,7 @@ def tile_gatedmultiscaleretentionlayer_pa_kernel(tc, x, ret_cat, Wg, bg, Wo, bo,
             cols = slice(16 * j, 16 * j + 16)
             steps = [
                 lambda: nc.vector.scalar_tensor_tensor(
-                    out=shift[:, cols], in0=sums[j][:, :, 0], scalar=-0.5, in1=rstd[:, cols], op0=ALU.mult, op1=ALU.mult
+                    out=shift[:, cols], in0=by_head(j, 1), scalar=-1.0, in1=rstd[:, cols], op0=ALU.mult, op1=ALU.mult
                 )
             ]
             if j < 3:
@@ -398,16 +389,13 @@ def tile_gatedmultiscaleretentionlayer_pa_kernel(tc, x, ret_cat, Wg, bg, Wo, bo,
         cat_transpose(1, 1)
         gate_silu(0, 7)
         multiply(0, 0)
-        last_join[1]()
         cat_transpose(2, 0)
         cat_transpose(2, 1)
         regroup(on_scalar, "wo", 1, 0)
         multiply(0, 1)
-        last_join[2]()
         cat_transpose(3, 0)
         cat_transpose(3, 1)
         multiply(1, 0)
-        last_join[3]()
         gate_matmuls(1, 0)
         multiply(1, 1)
         gate_matmuls(1, 1)
@@ -434,7 +422,6 @@ def tile_gatedmultiscaleretentionlayer_pa_kernel(tc, x, ret_cat, Wg, bg, Wo, bo,
         gate_silu(1, 4)
         out_matmuls(0, 1)
         gate_silu(1, 5)
-        last_join[4]()
         root(3)
         out_bias(0, 0)
         out_matmuls(1, 0)

@@ -34,69 +34,70 @@ def tile_gatedmultiscaleretentionlayer_pa_kernel(tc, x, ret_cat, Wg, bg, Wo, bo,
         stat = ctx.enter_context(tc.tile_pool(name="stat", bufs=1))
         cat_pool = ctx.enter_context(tc.tile_pool(name="cat", bufs=8))
         gate_pool = ctx.enter_context(tc.tile_pool(name="gate", bufs=1))
-        out_pool = ctx.enter_context(tc.tile_pool(name="out", bufs=4))
+        out_pool = ctx.enter_context(tc.tile_pool(name="out", bufs=8))
         psum = ctx.enter_context(tc.psum_pool(name="psum", bufs=1))
         ctx.enter_context(tc.manual_schedule())
 
         banks_taken = [0]
 
-        def bank():
+        def bank(dtype=F32):
             k = banks_taken[0] % BANKS
             banks_taken[0] += 1
-            return psum.tile([P, 512], F32, name="bank%d" % k)
+            return psum.tile([P, 2048 // (4 if dtype == F32 else 2)], dtype, name="bank%d" % k)
 
         identity = const.tile([P, P], F32, name="identity")
         make_identity(nc, identity[:])
+        identity16 = const.tile([P, P], BF16, name="identity16")
+        make_identity(nc, identity16[:])
         bg_rows = const.tile([P, P], BF16, name="bg_rows")
         nc.vector.memset(bg_rows[:], 0.0)
-        bo_row = const.tile([P, 1024], BF16, name="bo_row")
-        nc.vector.memset(bo_row[:], 0.0)
-        ones = const.tile([P, P], BF16, name="ones")
-        nc.vector.memset(ones[:], 1.0)
-        minus_half = const.tile([P, 2 * HEADS], F32, name="minus_half")
-        nc.vector.memset(minus_half[:], -0.5)
         ones_col = const.tile([P, 1], F32, name="ones_col")
         nc.vector.memset(ones_col[:], 1.0)
-        nc.scalar.dma_start(out=bg_rows[0:HEADS, :], in_=bg.rearrange("(c p) -> c p", p=P))
-        nc.scalar.dma_start(out=bo_row[0:1, :], in_=bo.rearrange("(o d) -> o d", o=1))
         scratch = const.tile([P, 1], F32, name="scratch")
-        nc.scalar.activation(out=scratch[:], in_=ones_col[:], func=ACT.Sqrt)
+
+        def load_table(func):
+            nc.scalar.activation(out=scratch[:], in_=ones_col[:], func=func)
 
         r_raw = [raw.tile([P, 1024], BF16, name="r_raw%d" % i) for i in range(8)]
         x_raw = [raw.tile([P, 2, 1024], BF16, name="x_raw%d" % j) for j in range(4)]
-        w_raw = {(w, g): raw.tile([P, 4, 1024], BF16, name="%s_raw%d" % (w, g)) for w in ("wg", "wo") for g in range(2)}
+        pieces = [(w, g, h) for w in ("wg", "wo") for g in range(2) for h in range(2)]
+        w_raw = {k: raw.tile([P, 4, 512], BF16, name="%s_raw%d%d" % k) for k in pieces}
 
-        def load(what, a, h=0):
+        def load_r(i):
+            nc.sync.dma_start(out=r_raw[i][:], in_=r_tiles[:, i, :])
+
+        def load_x(j):
+            nc.sync.dma_start(out=x_raw[j][:], in_=x_tiles[:, 2 * j : 2 * j + 2, :])
+
+        def load_w(w, g, h):
             cols = slice(512 * h, 512 * h + 512)
-            if what == "r":
-                nc.sync.dma_start(out=r_raw[a][:], in_=r_tiles[:, a, :])
-            elif what == "x":
-                nc.sync.dma_start(out=x_raw[a][:], in_=x_tiles[:, 2 * a : 2 * a + 2, :])
-            elif what == "wg":
+            if w == "wg":
                 for u in range(2):
-                    rows = slice(512 * a + 256 * u, 512 * a + 256 * u + 256)
+                    rows = slice(512 * g + 256 * u, 512 * g + 256 * u + 256)
                     nc.sync.dma_start(
-                        out=w_raw[("wg", a)][:, 2 * u : 2 * u + 2, cols],
+                        out=w_raw[(w, g, h)][:, 2 * u : 2 * u + 2, :],
                         in_=Wg[rows, cols].rearrange("(p e) n -> p e n", e=2),
                     )
             else:
                 nc.sync.dma_start(
-                    out=w_raw[("wo", a)][:, :, cols],
-                    in_=Wo[512 * a : 512 * a + 512, cols].rearrange("(t p) n -> p t n", p=P),
+                    out=w_raw[(w, g, h)][:],
+                    in_=Wo[512 * g : 512 * g + 512, cols].rearrange("(t p) n -> p t n", p=P),
                 )
 
-        bg_rows32 = const.tile([P, P], F32, name="bg_rows32")
-        nc.vector.tensor_copy(out=bg_rows32[:], in_=bg_rows[:])
-        bg_bank = bank()
-        nc.tensor.transpose(bg_bank[:, 0:P], bg_rows32[:], identity[:])
+        def load_bg():
+            nc.scalar.dma_start(out=bg_rows[0:HEADS, :], in_=bg.rearrange("(c p) -> c p", p=P))
+
+        bo_all = const.tile([P, 1024], BF16, name="bo_all")
+
+        def load_bo():
+            nc.sync.dma_start(out=bo_all[:], in_=bo.partition_broadcast(P))
+
         bg_col = const.tile([P, HEADS], F32, name="bg_col")
-        nc.vector.tensor_copy(out=bg_col[:], in_=bg_bank[:, 0:HEADS])
-        bo_all = const.tile([P, 1024], F32, name="bo_all")
-        for h in range(2):
-            cols = slice(512 * h, 512 * h + 512)
-            bo_bank = bank()
-            nc.tensor.matmul(bo_bank[:], lhsT=ones[:], rhs=bo_row[:, cols], start=True, stop=True)
-            nc.scalar.copy(out=bo_all[:, cols], in_=bo_bank[:])
+
+        def bg_columns():
+            bg_bank = bank(BF16)
+            nc.tensor.transpose(bg_bank[:, 0:P], bg_rows[:], identity16[:])
+            nc.scalar.copy(out=bg_col[:], in_=bg_bank[:, 0:HEADS])
 
         def mx_operand(name):
             return (
@@ -105,7 +106,7 @@ def tile_gatedmultiscaleretentionlayer_pa_kernel(tc, x, ret_cat, Wg, bg, Wo, bo,
             )
 
         x_mx = {(g, b): mx_operand("x%d%d" % (g, b)) for g in range(2) for b in range(2)}
-        w_mx = {(w, g, h): mx_operand("%s%d%d" % (w, g, h)) for w in ("wg", "wo") for g in range(2) for h in range(2)}
+        w_mx = {k: mx_operand("%s%d%d" % k) for k in pieces}
         h_mx = {(g, b): mx_operand("h%d%d" % (g, b)) for g in range(2) for b in range(2)}
 
         def grouped_tile(tag, bufs):
@@ -130,68 +131,77 @@ def tile_gatedmultiscaleretentionlayer_pa_kernel(tc, x, ret_cat, Wg, bg, Wo, bo,
                     stop=(g == 1),
                 )
 
-        def weave(long_steps, short_steps, places):
-            for k, step in enumerate(long_steps):
-                step()
-                for place, short in zip(places, short_steps):
-                    if place == k:
-                        short()
-
-        rstd = stat.tile([P, 64], F32, name="rstd")
-        shift = stat.tile([P, 64], F32, name="shift")
         moments = [stat.tile([P, HEADS, 6], F32, name="moments%d" % j) for j in range(4)]
-        var_eps = [stat.tile([P, 2 * HEADS], F32, name="var_eps%d" % j) for j in range(4)]
+        rstd = [stat.tile([P, 2 * HEADS], F32, name="rstd%d" % j) for j in range(4)]
 
-        def by_head(j, k):
-            return moments[j][:].rearrange("p n (a k) -> p (n a) k", a=2)[:, :, k]
-
-        def statistics(i, short_steps=()):
-            def two_heads(n):
-                return lambda: nc.vector.bn_stats(
+        def statistics(i):
+            for n in range(4):
+                nc.vector.bn_stats(
                     out=moments[i // 2][:, 4 * (i % 2) + n, :],
                     in_=r_raw[i][:, 2 * P * n : 2 * P * n + 2 * P].rearrange("p (a k) -> p k a", a=2),
                 )
 
-            weave([two_heads(n) for n in range(4)], short_steps, (0, 2))
+        minus_half = const.tile([P, 2 * HEADS], F32, name="minus_half")
+        nc.vector.memset(minus_half[:], -0.5)
+        var_eps = stat.tile([P, 2 * HEADS], F32, name="var_eps")
 
-        def join(j):
-            return [
-                lambda: nc.vector.tensor_scalar(
-                    out=var_eps[j][:], in0=by_head(j, 2), scalar1=1.0 / P, scalar2=EPS, op0=ALU.mult, op1=ALU.add
-                ),
-            ]
-
-        std = [stat.tile([P, 2 * HEADS], F32, name="std%d" % j) for j in range(3)]
+        def last_root():
+            nc.vector.tensor_scalar(
+                out=var_eps[:],
+                in0=moments[3][:].rearrange("p n (a k) -> p (n a) k", a=2)[:, :, 2],
+                scalar1=1.0 / P,
+                scalar2=EPS,
+                op0=ALU.mult,
+                op1=ALU.add,
+            )
+            nc.gpsimd.tensor_tensor(out=rstd[3][:], in0=var_eps[:], in1=minus_half[:], op=ALU.pow)
 
         def root(j):
-            if j < 3:
-                nc.scalar.activation(out=std[j][:], in_=var_eps[j][:], func=ACT.Sqrt)
-            else:
-                nc.gpsimd.tensor_tensor(out=rstd[:, 48:64], in0=var_eps[j][:], in1=minus_half[:], op=ALU.pow)
+            nc.scalar.activation(
+                out=rstd[j][:],
+                in_=moments[j][:].rearrange("p n (a k) -> p (n a) k", a=2)[:, :, 2],
+                func=ACT.Abs_reciprocal_sqrt,
+                scale=1.0 / P,
+                bias=EPS,
+            )
+
+        shift = [stat.tile([P, 2 * HEADS], F32, name="shift%d" % j) for j in range(4)]
 
         def finish(j):
-            cols = slice(16 * j, 16 * j + 16)
-            steps = [
-                lambda: nc.vector.scalar_tensor_tensor(
-                    out=shift[:, cols], in0=by_head(j, 1), scalar=-1.0, in1=rstd[:, cols], op0=ALU.mult, op1=ALU.mult
-                )
-            ]
-            if j < 3:
-                steps = [lambda: nc.vector.reciprocal(out=rstd[:, cols], in_=std[j][:])] + steps
-            return steps
+            nc.vector.scalar_tensor_tensor(
+                out=shift[j][:],
+                in0=moments[j][:].rearrange("p n (a k) -> p (n a) k", a=2)[:, :, 1],
+                scalar=-1.0,
+                in1=rstd[j][:],
+                op0=ALU.mult,
+                op1=ALU.mult,
+            )
 
         cat = {}
 
         def normalise(i):
             cat[i] = cat_pool.tile([P, 1024], F32, name="cat")
             for c in range(HEADS):
-                col = HEADS * i + c
+                col = HEADS * (i % 2) + c
                 nc.scalar.activation(
                     out=cat[i][:, P * c : P * c + P],
                     in_=r_raw[i][:, P * c : P * c + P],
                     func=ACT.Identity,
-                    bias=shift[:, col : col + 1],
-                    scale=rstd[:, col : col + 1],
+                    bias=shift[i // 2][:, col : col + 1],
+                    scale=rstd[i // 2][:, col : col + 1],
+                )
+
+        def normalise_on_vector(i):
+            cat[i] = cat_pool.tile([P, 1024], F32, name="cat")
+            for c in range(HEADS):
+                col = HEADS * (i % 2) + c
+                nc.vector.tensor_scalar(
+                    out=cat[i][:, P * c : P * c + P],
+                    in0=r_raw[i][:, P * c : P * c + P],
+                    scalar1=rstd[i // 2][:, col : col + 1],
+                    scalar2=shift[i // 2][:, col : col + 1],
+                    op0=ALU.mult,
+                    op1=ALU.add,
                 )
 
         x_bank = {}
@@ -215,9 +225,8 @@ def tile_gatedmultiscaleretentionlayer_pa_kernel(tc, x, ret_cat, Wg, bg, Wo, bo,
                     in_=x_bank[i][:, 256 * g : 256 * g + 256].rearrange("p (u r) -> p r u", u=2),
                 )
 
-        def x_quantise(b):
-            for g in range(2):
-                quantise(x_mx[(g, b)], x_grouped[(g, b)])
+        def x_quantise(b, g):
+            quantise(x_mx[(g, b)], x_grouped[(g, b)])
 
         w_grouped = {}
 
@@ -225,8 +234,22 @@ def tile_gatedmultiscaleretentionlayer_pa_kernel(tc, x, ret_cat, Wg, bg, Wo, bo,
             w_grouped[(w, g, h)] = grouped_tile("w%d%d" % (g, h), 1)
             copy(
                 out=w_grouped[(w, g, h)][:].rearrange("p (c i t) -> p c t i", i=4, t=4),
-                in_=w_raw[(w, g)][:, :, 512 * h : 512 * h + 512].rearrange("p t (c i) -> p c t i", i=4),
+                in_=w_raw[(w, g, h)][:].rearrange("p t (c i) -> p c t i", i=4),
             )
+
+        def regroup_by_tensor(w, g, h):
+            w_grouped[(w, g, h)] = grouped_tile("w%d%d" % (g, h), 1)
+            for q in range(2):
+                words = bank(BF16)
+                for u in range(2):
+                    nc.tensor.matmul(
+                        words[:].rearrange("p (n u e) -> p u n e", u=2, e=2)[:, u],
+                        lhsT=identity16[:],
+                        rhs=w_raw[(w, g, h)][:, 2 * u : 2 * u + 2, 256 * q : 256 * q + 256].rearrange("p e n -> p n e"),
+                        start=True,
+                        stop=True,
+                    )
+                nc.scalar.copy(out=w_grouped[(w, g, h)][:, 1024 * q : 1024 * q + 1024], in_=words[:])
 
         def w_quantise(w, g, h):
             quantise(w_mx[(w, g, h)], w_grouped[(w, g, h)])
@@ -268,7 +291,7 @@ def tile_gatedmultiscaleretentionlayer_pa_kernel(tc, x, ret_cat, Wg, bg, Wo, bo,
 
         def multiply(i, g):
             b, place = i // 4, i % 4
-            if place == 0:
+            if (g, b) not in h_grouped:
                 h_grouped[(g, b)] = grouped_tile("x_or_h", 4)
             nc.vector.tensor_tensor(
                 out=h_grouped[(g, b)][:, 512 * place : 512 * place + 512].rearrange("p (c i t) -> p c t i", i=4, t=4),
@@ -277,12 +300,10 @@ def tile_gatedmultiscaleretentionlayer_pa_kernel(tc, x, ret_cat, Wg, bg, Wo, bo,
                 op=ALU.mult,
             )
 
-        def h_quantise(b, half):
-            for g in range(2):
-                quantise(h_mx[(g, b)], h_grouped[(g, b)], 256 * half, 256)
+        def h_quantise(b, half, g):
+            quantise(h_mx[(g, b)], h_grouped[(g, b)], 256 * half, 256)
 
         out_bank = {}
-        out_tile = {}
 
         def out_matmuls(i, h):
             out_bank[(i, h)] = bank()
@@ -295,186 +316,148 @@ def tile_gatedmultiscaleretentionlayer_pa_kernel(tc, x, ret_cat, Wg, bg, Wo, bo,
             )
 
         def out_bias(i, h):
-            if h == 0:
-                out_tile[i] = out_pool.tile([P, 1024], F32, name="out_tile")
+            result = out_pool.tile([P, 512], F32, name="result")
             cols = slice(512 * h, 512 * h + 512)
-            nc.vector.tensor_tensor(out=out_tile[i][:, cols], in0=out_bank[(i, h)][:], in1=bo_all[:, cols], op=ALU.add)
-            nc.sync.dma_start(out=out_tiles[:, i, cols], in_=out_tile[i][:, cols])
+            nc.vector.tensor_tensor(out=result[:], in0=out_bank[(i, h)][:], in1=bo_all[:, cols], op=ALU.add)
+            nc.sync.dma_start(out=out_tiles[:, i, cols], in_=result[:])
 
-        load("r", 0)
-        load("wg", 0, 0)
-        load("r", 1)
-        load("wg", 0, 1)
-        load("r", 2)
-        load("x", 0)
-        load("x", 1)
-        load("r", 3)
-        load("wo", 0, 0)
+        load_bg()
+        load_table(ACT.Abs_reciprocal_sqrt)
+        load_r(0)
+        load_r(1)
+        load_w("wg", 0, 0)
+        load_r(2)
+        load_x(0)
+        load_r(3)
+        load_w("wg", 1, 0)
+        load_r(4)
+        load_x(1)
+        load_w("wg", 0, 1)
+        load_r(5)
+        load_w("wg", 1, 1)
+        load_r(6)
+        load_r(7)
+        load_x(2)
+        load_x(3)
+        for h in range(2):
+            for g in range(2):
+                load_w("wo", g, h)
+        load_bo()
+
         statistics(0)
-        load("r", 4)
-        regroup(on_scalar, "wg", 0, 0)
-        load("wg", 1, 0)
         statistics(1)
-        load("x", 2)
-        load("r", 5)
-        regroup(on_scalar, "wg", 0, 1)
-        statistics(2, join(0))
-        load("x", 3)
-        x_transpose(0)
-        load("wg", 1, 1)
-        w_quantise("wg", 0, 0)
-        x_transpose(1)
+        regroup_by_tensor("wg", 0, 0)
         root(0)
+        statistics(2)
+        finish(0)
+        x_transpose(0)
+        x_transpose(1)
         x_copy(0)
-        x_transpose(2)
-        load("wo", 1, 1)
         x_copy(1)
+        statistics(3)
+        normalise(0)
+        root(1)
+        w_quantise("wg", 0, 0)
+        regroup_by_tensor("wg", 1, 0)
+        statistics(4)
+        finish(1)
+        x_transpose(2)
         x_transpose(3)
-        statistics(3, finish(0))
-        load("r", 6)
         x_copy(2)
         x_copy(3)
-        load("r", 7)
-        regroup(on_scalar, "wo", 0, 0)
-        statistics(4, join(1))
-        load("wo", 1, 0)
-        load("wo", 0, 1)
-        x_quantise(0)
-        normalise(0)
-        x_transpose(4)
-        regroup(on_vector, "wg", 1, 0)
-        x_transpose(5)
-        root(1)
-        normalise(1)
-        w_quantise("wg", 0, 1)
-        x_transpose(6)
-        statistics(5, finish(1))
-        x_copy(4)
-        x_transpose(7)
-        x_copy(5)
-        x_copy(6)
-        w_quantise("wo", 0, 0)
-        x_copy(7)
+        bg_columns()
+        regroup_by_tensor("wg", 0, 1)
+        statistics(5)
         w_quantise("wg", 1, 0)
-        normalise(2)
-        statistics(6, join(2))
-        gate_matmuls(0, 0)
-        normalise(3)
-        gate_matmuls(0, 1)
-        regroup(on_vector, "wg", 1, 1)
-        gate_matmuls(0, 2)
-        gate_matmuls(0, 3)
         root(2)
-        gate_silu(0, 0)
+        x_quantise(0, 0)
+        regroup_by_tensor("wg", 1, 1)
+        finish(2)
+        x_quantise(0, 1)
+        load_table(ACT.Silu)
+        for c in range(4):
+            gate_matmuls(0, c)
+        normalise_on_vector(1)
+        w_quantise("wg", 0, 1)
+        normalise_on_vector(2)
+        normalise_on_vector(3)
         w_quantise("wg", 1, 1)
-        statistics(7, finish(2))
-        gate_matmuls(0, 4)
-        gate_silu(0, 1)
-        gate_matmuls(0, 5)
-        x_quantise(1)
-        gate_matmuls(0, 6)
-        gate_silu(0, 2)
-        gate_matmuls(0, 7)
-        gate_silu(0, 3)
-        regroup(on_vector, "wo", 1, 1)
-        cat_transpose(0, 0)
-        gate_silu(0, 4)
-        cat_transpose(0, 1)
-        gate_silu(0, 5)
-        last_join = join(3)
-        cat_transpose(1, 0)
-        gate_silu(0, 6)
-        w_quantise("wo", 1, 1)
-        last_join[0]()
-        cat_transpose(1, 1)
-        gate_silu(0, 7)
-        multiply(0, 0)
-        cat_transpose(2, 0)
-        cat_transpose(2, 1)
-        regroup(on_scalar, "wo", 1, 0)
-        multiply(0, 1)
-        cat_transpose(3, 0)
-        cat_transpose(3, 1)
-        multiply(1, 0)
-        gate_matmuls(1, 0)
-        multiply(1, 1)
-        gate_matmuls(1, 1)
-        h_quantise(0, 0)
-        regroup(on_scalar, "wo", 0, 1)
-        gate_matmuls(1, 2)
-        multiply(2, 0)
-        gate_matmuls(1, 3)
-        multiply(2, 1)
-        gate_matmuls(1, 4)
-        w_quantise("wo", 1, 0)
-        gate_matmuls(1, 5)
-        gate_silu(1, 0)
-        multiply(3, 0)
-        gate_silu(1, 1)
-        multiply(3, 1)
-        gate_matmuls(1, 6)
-        gate_silu(1, 2)
-        w_quantise("wo", 0, 1)
-        gate_matmuls(1, 7)
-        gate_silu(1, 3)
-        h_quantise(0, 1)
-        out_matmuls(0, 0)
-        gate_silu(1, 4)
-        out_matmuls(0, 1)
-        gate_silu(1, 5)
-        root(3)
-        out_bias(0, 0)
-        out_matmuls(1, 0)
-        gate_silu(1, 6)
-        out_bias(0, 1)
-        out_matmuls(1, 1)
-        gate_silu(1, 7)
-        out_bias(1, 0)
-        out_matmuls(2, 0)
+        for c in range(4):
+            gate_silu(0, c)
+        statistics(6)
+        for i in range(4):
+            cat_transpose(i, 0)
+        for c in range(4, 8):
+            gate_matmuls(0, c)
+        statistics(7)
+        for c in range(4, 8):
+            gate_silu(0, c)
+        last_root()
+        for i in range(4):
+            multiply(i, 0)
+        for i in range(4):
+            cat_transpose(i, 1)
+        for i in range(4, 8):
+            x_transpose(i)
+        for i in range(4, 8):
+            x_copy(i)
+        for i in range(4):
+            multiply(i, 1)
+        for g in range(2):
+            x_quantise(1, g)
+        finish(3)
+        for c in range(4):
+            gate_matmuls(1, c)
         normalise(4)
-        out_bias(1, 1)
-        out_matmuls(2, 1)
-        out_bias(2, 0)
-        out_matmuls(3, 0)
-        out_bias(2, 1)
-        out_matmuls(3, 1)
         normalise(5)
-        out_bias(3, 0)
-        finish(3)[0]()
-        cat_transpose(4, 0)
-        out_bias(3, 1)
-        cat_transpose(4, 1)
+        regroup(on_vector, "wo", 0, 0)
+        for c in range(4):
+            gate_silu(1, c)
+        for g in range(2):
+            for half in range(2):
+                h_quantise(0, half, g)
+        regroup(on_vector, "wo", 1, 0)
+        for c in range(4, 8):
+            gate_matmuls(1, c)
+        w_quantise("wo", 0, 0)
         normalise(6)
-        multiply(4, 0)
-        cat_transpose(5, 0)
-        cat_transpose(5, 1)
-        multiply(4, 1)
+        w_quantise("wo", 1, 0)
         normalise(7)
-        multiply(5, 0)
-        cat_transpose(6, 0)
-        multiply(5, 1)
-        cat_transpose(6, 1)
-        h_quantise(1, 0)
-        cat_transpose(7, 0)
-        multiply(6, 0)
-        cat_transpose(7, 1)
+        for i in range(4, 8):
+            cat_transpose(i, 0)
+        for c in range(4, 8):
+            gate_silu(1, c)
+        for i in range(4):
+            out_matmuls(i, 0)
+        for i in range(4, 8):
+            multiply(i, 0)
+        regroup(on_scalar, "wo", 0, 1)
+        for i in range(4, 8):
+            cat_transpose(i, 1)
+        for i in range(4):
+            out_bias(i, 0)
+        regroup(on_scalar, "wo", 1, 1)
+        for i in range(4, 6):
+            multiply(i, 1)
+        h_quantise(1, 0, 0)
         multiply(6, 1)
-        out_matmuls(4, 0)
-        multiply(7, 0)
-        out_matmuls(4, 1)
+        h_quantise(1, 0, 1)
         multiply(7, 1)
-        out_matmuls(5, 0)
-        h_quantise(1, 1)
-        out_matmuls(5, 1)
-        out_bias(4, 0)
-        out_matmuls(6, 0)
-        out_bias(4, 1)
-        out_matmuls(6, 1)
-        out_bias(5, 0)
-        out_matmuls(7, 0)
-        out_bias(5, 1)
-        out_matmuls(7, 1)
-        out_bias(6, 0)
-        out_bias(6, 1)
-        out_bias(7, 0)
-        out_bias(7, 1)
+        h_quantise(1, 1, 0)
+        for i in range(4, 6):
+            out_matmuls(i, 0)
+        w_quantise("wo", 0, 1)
+        h_quantise(1, 1, 1)
+        for i in range(4, 6):
+            out_bias(i, 0)
+        w_quantise("wo", 1, 1)
+        for i in range(6, 8):
+            out_matmuls(i, 0)
+        for i in range(4):
+            out_matmuls(i, 1)
+        for i in range(6, 8):
+            out_bias(i, 0)
+        for i in range(4, 8):
+            out_matmuls(i, 1)
+        for i in range(8):
+            out_bias(i, 1)

@@ -338,124 +338,115 @@ def tile_gatedmultiscaleretentionlayer_pa_kernel(tc, x, ret_cat, Wg, bg, Wo, bo,
         load_r(6)
         load_r(7)
         load_x(2)
+        load_w("wo", 0, 0)
         load_x(3)
-        for h in range(2):
-            for g in range(2):
-                load_w("wo", g, h)
+        load_w("wo", 1, 0)
+        load_w("wo", 0, 1)
+        load_w("wo", 1, 1)
         load_bo()
 
         statistics(0)
-        statistics(1)
         regroup_by_tensor("wg", 0, 0)
-        root(0)
-        statistics(2)
-        finish(0)
         x_transpose(0)
         x_transpose(1)
+        statistics(1)
+        root(0)
         x_copy(0)
         x_copy(1)
-        statistics(3)
-        normalise(0)
-        root(1)
-        w_quantise("wg", 0, 0)
+        statistics(2)
         regroup_by_tensor("wg", 1, 0)
-        statistics(4)
-        finish(1)
         x_transpose(2)
         x_transpose(3)
+        statistics(3)
+        finish(0)
+        w_quantise("wg", 0, 0)
+        root(1)
+        normalise_on_vector(1)
         x_copy(2)
         x_copy(3)
         bg_columns()
         regroup_by_tensor("wg", 0, 1)
-        statistics(5)
+        statistics(4)
         w_quantise("wg", 1, 0)
-        root(2)
-        x_quantise(0, 0)
+        finish(1)
+        for g in range(2):
+            x_quantise(0, g)
+        normalise(0)
         regroup_by_tensor("wg", 1, 1)
-        finish(2)
-        x_quantise(0, 1)
-        load_table(ACT.Silu)
         for c in range(4):
             gate_matmuls(0, c)
-        normalise_on_vector(1)
+        statistics(5)
+        root(2)
+        load_table(ACT.Silu)
         w_quantise("wg", 0, 1)
-        normalise_on_vector(2)
-        normalise_on_vector(3)
-        w_quantise("wg", 1, 1)
-        for c in range(4):
-            gate_silu(0, c)
         statistics(6)
-        for i in range(4):
-            cat_transpose(i, 0)
+        w_quantise("wg", 1, 1)
         for c in range(4, 8):
             gate_matmuls(0, c)
         statistics(7)
-        for c in range(4, 8):
+        for c in range(8):
             gate_silu(0, c)
+        finish(2)
         last_root()
-        for i in range(4):
-            multiply(i, 0)
-        for i in range(4):
-            cat_transpose(i, 1)
+        normalise_on_vector(2)
+        normalise_on_vector(3)
+        for g in range(2):
+            for i in range(4):
+                cat_transpose(i, g)
+        for g in range(2):
+            for i in range(4):
+                multiply(i, g)
         for i in range(4, 8):
             x_transpose(i)
+        normalise(4)
         for i in range(4, 8):
             x_copy(i)
-        for i in range(4):
-            multiply(i, 1)
+        finish(3)
         for g in range(2):
             x_quantise(1, g)
-        finish(3)
+        normalise(5)
         for c in range(4):
             gate_matmuls(1, c)
-        normalise(4)
-        normalise(5)
         regroup(on_vector, "wo", 0, 0)
         for c in range(4):
             gate_silu(1, c)
+        normalise_on_vector(7)
+        normalise(6)
+        regroup(on_vector, "wo", 1, 0)
+        for i in range(4, 8):
+            cat_transpose(i, 0)
+        for g in range(2):
+            w_quantise("wo", g, 0)
+        for c in range(4, 8):
+            gate_matmuls(1, c)
         for g in range(2):
             for half in range(2):
                 h_quantise(0, half, g)
-        regroup(on_vector, "wo", 1, 0)
-        for c in range(4, 8):
-            gate_matmuls(1, c)
-        w_quantise("wo", 0, 0)
-        normalise(6)
-        w_quantise("wo", 1, 0)
-        normalise(7)
-        for i in range(4, 8):
-            cat_transpose(i, 0)
         for c in range(4, 8):
             gate_silu(1, c)
-        for i in range(4):
-            out_matmuls(i, 0)
         for i in range(4, 8):
             multiply(i, 0)
-        regroup(on_scalar, "wo", 0, 1)
         for i in range(4, 8):
             cat_transpose(i, 1)
-        for i in range(4):
-            out_bias(i, 0)
+        regroup(on_scalar, "wo", 0, 1)
+        for half in range(2):
+            h_quantise(1, half, 0)
         regroup(on_scalar, "wo", 1, 1)
-        for i in range(4, 6):
+        for i in range(4, 8):
             multiply(i, 1)
-        h_quantise(1, 0, 0)
-        multiply(6, 1)
-        h_quantise(1, 0, 1)
-        multiply(7, 1)
-        h_quantise(1, 1, 0)
-        for i in range(4, 6):
+        for i in range(4):
             out_matmuls(i, 0)
         w_quantise("wo", 0, 1)
-        h_quantise(1, 1, 1)
-        for i in range(4, 6):
+        for half in range(2):
+            h_quantise(1, half, 1)
+        for i in range(4):
             out_bias(i, 0)
         w_quantise("wo", 1, 1)
-        for i in range(6, 8):
+        for i in range(4, 8):
             out_matmuls(i, 0)
         for i in range(4):
             out_matmuls(i, 1)
-        for i in range(6, 8):
+        for i in range(4, 8):
             out_bias(i, 0)
         for i in range(4, 8):
             out_matmuls(i, 1)

@@ -327,8 +327,8 @@ def tile_gatedmultiscaleretentionlayer_pa_kernel(tc, x, ret_cat, Wg, bg, Wo, bo,
         load_r(1)
         load_w("wg", 0, 0)
         load_r(2)
-        load_x(0)
         load_r(3)
+        load_x(0)
         load_w("wg", 1, 0)
         load_r(4)
         load_x(1)
@@ -344,24 +344,24 @@ def tile_gatedmultiscaleretentionlayer_pa_kernel(tc, x, ret_cat, Wg, bg, Wo, bo,
         load_w("wo", 0, 1)
         load_w("wo", 1, 1)
         load_bo()
-
         statistics(0)
+        statistics(1)
+        root(0)
+        statistics(2)
+        finish(0)
+        normalise(0)
         regroup_by_tensor("wg", 0, 0)
         x_transpose(0)
         x_transpose(1)
-        statistics(1)
-        root(0)
         x_copy(0)
         x_copy(1)
-        statistics(2)
         regroup_by_tensor("wg", 1, 0)
         x_transpose(2)
         x_transpose(3)
         statistics(3)
-        finish(0)
+        normalise_on_vector(1)
         w_quantise("wg", 0, 0)
         root(1)
-        normalise_on_vector(1)
         x_copy(2)
         x_copy(3)
         bg_columns()
@@ -371,16 +371,16 @@ def tile_gatedmultiscaleretentionlayer_pa_kernel(tc, x, ret_cat, Wg, bg, Wo, bo,
         finish(1)
         for g in range(2):
             x_quantise(0, g)
-        normalise(0)
-        regroup_by_tensor("wg", 1, 1)
         for c in range(4):
             gate_matmuls(0, c)
         statistics(5)
+        normalise(2)
         root(2)
         load_table(ACT.Silu)
         w_quantise("wg", 0, 1)
-        statistics(6)
+        regroup(on_vector, "wg", 1, 1)
         w_quantise("wg", 1, 1)
+        statistics(6)
         for c in range(4, 8):
             gate_matmuls(0, c)
         statistics(7)
@@ -388,7 +388,6 @@ def tile_gatedmultiscaleretentionlayer_pa_kernel(tc, x, ret_cat, Wg, bg, Wo, bo,
             gate_silu(0, c)
         finish(2)
         last_root()
-        normalise_on_vector(2)
         normalise_on_vector(3)
         for g in range(2):
             for i in range(4):
@@ -432,21 +431,27 @@ def tile_gatedmultiscaleretentionlayer_pa_kernel(tc, x, ret_cat, Wg, bg, Wo, bo,
         for half in range(2):
             h_quantise(1, half, 0)
         regroup(on_scalar, "wo", 1, 1)
-        for i in range(4, 8):
-            multiply(i, 1)
         for i in range(4):
             out_matmuls(i, 0)
-        w_quantise("wo", 0, 1)
+        for i in range(4, 6):
+            multiply(i, 1)
+        for i in range(2):
+            out_bias(i, 0)
+        for i in range(6, 8):
+            multiply(i, 1)
         for half in range(2):
             h_quantise(1, half, 1)
-        for i in range(4):
+        for i in range(2, 4):
             out_bias(i, 0)
-        w_quantise("wo", 1, 1)
         for i in range(4, 8):
             out_matmuls(i, 0)
+        for i in range(4, 6):
+            out_bias(i, 0)
+        for g in range(2):
+            w_quantise("wo", g, 1)
         for i in range(4):
             out_matmuls(i, 1)
-        for i in range(4, 8):
+        for i in range(6, 8):
             out_bias(i, 0)
         for i in range(4, 8):
             out_matmuls(i, 1)

@@ -431,27 +431,21 @@ def tile_gatedmultiscaleretentionlayer_pa_kernel(tc, x, ret_cat, Wg, bg, Wo, bo,
         for half in range(2):
             h_quantise(1, half, 0)
         regroup(on_scalar, "wo", 1, 1)
+        for i in range(4, 8):
+            multiply(i, 1)
         for i in range(4):
             out_matmuls(i, 0)
-        for i in range(4, 6):
-            multiply(i, 1)
-        for i in range(2):
-            out_bias(i, 0)
-        for i in range(6, 8):
-            multiply(i, 1)
+        w_quantise("wo", 0, 1)
         for half in range(2):
             h_quantise(1, half, 1)
-        for i in range(2, 4):
+        for i in range(4):
             out_bias(i, 0)
+        w_quantise("wo", 1, 1)
         for i in range(4, 8):
             out_matmuls(i, 0)
-        for i in range(4, 6):
-            out_bias(i, 0)
-        for g in range(2):
-            w_quantise("wo", g, 1)
         for i in range(4):
             out_matmuls(i, 1)
-        for i in range(6, 8):
+        for i in range(4, 8):
             out_bias(i, 0)
         for i in range(4, 8):
             out_matmuls(i, 1)

from contextlib import ExitStack

import concourse.mybir as mybir
from concourse.masks import make_identity

FLOPS = 2 * 2 * 1024 * 1024 * 1024

BF16 = mybir.dt.bfloat16
F32 = mybir.dt.float32
U32 = mybir.dt.uint32
U8 = mybir.dt.uint8
FP8X4 = mybir.dt.float8_e4m3fn_x4
ACT = mybir.ActivationFunctionType
ALU = mybir.AluOpType
AX = mybir.AxisListType

P = 128
HEADS = 8
EPS = 1e-5
BANKS = 8


def tile_gatedmultiscaleretentionlayer_pa_kernel(tc, x, ret_cat, Wg, bg, Wo, bo, out):
    nc = tc.nc
    x_tiles = x.flatten_outer_dims().rearrange("(p i) k -> p i k", i=8)
    r_tiles = ret_cat.flatten_outer_dims().rearrange("(p i) c -> p i c", i=8)
    out_tiles = out.flatten_outer_dims().rearrange("(p i) d -> p i d", i=8)

    with ExitStack() as ctx:
        const = ctx.enter_context(tc.tile_pool(name="const", bufs=1))
        raw = ctx.enter_context(tc.tile_pool(name="raw", bufs=1))
        grouped = ctx.enter_context(tc.tile_pool(name="grouped", bufs=1))
        packed = ctx.enter_context(tc.tile_pool(name="packed", bufs=1))
        stat = ctx.enter_context(tc.tile_pool(name="stat", bufs=1))
        cat_pool = ctx.enter_context(tc.tile_pool(name="cat", bufs=8))
        gate_pool = ctx.enter_context(tc.tile_pool(name="gate", bufs=1))
        out_pool = ctx.enter_context(tc.tile_pool(name="out", bufs=8))
        psum = ctx.enter_context(tc.psum_pool(name="psum", bufs=1))
        ctx.enter_context(tc.manual_schedule())

        banks_taken = [0]

        def bank(dtype=F32):
            k = banks_taken[0] % BANKS
            banks_taken[0] += 1
            return psum.tile([P, 2048 // (4 if dtype == F32 else 2)], dtype, name="bank%d" % k)

        identity = const.tile([P, P], F32, name="identity")
        make_identity(nc, identity[:])
        identity16 = const.tile([P, P], BF16, name="identity16")
        make_identity(nc, identity16[:])
        bg_rows = const.tile([P, P], BF16, name="bg_rows")
        nc.vector.memset(bg_rows[:], 0.0)
        ones_col = const.tile([P, 1], F32, name="ones_col")
        nc.vector.memset(ones_col[:], 1.0)
        scratch = const.tile([P, 1], F32, name="scratch")

        def load_table(func):
            nc.scalar.activation(out=scratch[:], in_=ones_col[:], func=func)

        r_raw = [raw.tile([P, 1024], BF16, name="r_raw%d" % i) for i in range(8)]
        x_raw = [raw.tile([P, 2, 1024], BF16, name="x_raw%d" % j) for j in range(4)]
        pieces = [(w, g, h) for w in ("wg", "wo") for g in range(2) for h in range(2)]
        w_raw = {k: raw.tile([P, 4, 512], BF16, name="%s_raw%d%d" % k) for k in pieces}

        def load_r(i):
            nc.sync.dma_start(out=r_raw[i][:], in_=r_tiles[:, i, :])

        def load_x(j):
            nc.sync.dma_start(out=x_raw[j][:], in_=x_tiles[:, 2 * j : 2 * j + 2, :])

        def load_w(w, g, h):
            cols = slice(512 * h, 512 * h + 512)
            if w == "wg":
                for u in range(2):
                    rows = slice(512 * g + 256 * u, 512 * g + 256 * u + 256)
                    nc.sync.dma_start(
                        out=w_raw[(w, g, h)][:, 2 * u : 2 * u + 2, :],
                        in_=Wg[rows, cols].rearrange("(p e) n -> p e n", e=2),
                    )
            else:
                nc.sync.dma_start(
                    out=w_raw[(w, g, h)][:],
                    in_=Wo[512 * g : 512 * g + 512, cols].rearrange("(t p) n -> p t n", p=P),
                )

        def load_bg():
            nc.scalar.dma_start(out=bg_rows[0:HEADS, :], in_=bg.rearrange("(c p) -> c p", p=P))

        bo_all = const.tile([P, 1024], BF16, name="bo_all")

        def load_bo():
            nc.sync.dma_start(out=bo_all[:], in_=bo.partition_broadcast(P))

        bg_col = const.tile([P, HEADS], F32, name="bg_col")

        def bg_columns():
            bg_bank = bank(BF16)
            nc.tensor.transpose(bg_bank[:, 0:P], bg_rows[:], identity16[:])
            nc.scalar.copy(out=bg_col[:], in_=bg_bank[:, 0:HEADS])

        def mx_operand(name):
            return (
                packed.tile([P, 512], U32, name=name + "_codes", align_bytes=64),
                packed.tile([P, 512], U8, name=name + "_scales", align_bytes=64),
            )

        x_mx = {(g, b): mx_operand("x%d%d" % (g, b)) for g in range(2) for b in range(2)}
        w_mx = {k: mx_operand("%s%d%d" % k) for k in pieces}
        h_mx = {(g, b): mx_operand("h%d%d" % (g, b)) for g in range(2) for b in range(2)}

        def grouped_tile(tag, bufs):
            return grouped.tile([P, 2048], BF16, name=tag, bufs=bufs, align_bytes=64)

        def quantise(operand, source, first=0, words=512):
            nc.vector.quantize_mx(
                out=operand[0][:, first : first + words].bitcast(FP8X4),
                scales=operand[1][:, first : first + words],
                in_=source[:, 4 * first : 4 * (first + words)],
            )

        def mx_group(acc, stationary, cols, moving):
            for g in range(2):
                nc.tensor.matmul_mx(
                    out=acc[:],
                    lhsT=stationary[g][0][:, cols].bitcast(FP8X4),
                    lhsT_scale=stationary[g][1][:, cols],
                    rhs=moving[g][0][:].bitcast(FP8X4),
                    rhs_scale=moving[g][1][:],
                    start=(g == 0),
                    stop=(g == 1),
                )

        moments = [stat.tile([P, HEADS, 6], F32, name="moments%d" % j) for j in range(4)]
        rstd = [stat.tile([P, 2 * HEADS], F32, name="rstd%d" % j) for j in range(4)]

        def statistics(i):
            for n in range(4):
                nc.vector.bn_stats(
                    out=moments[i // 2][:, 4 * (i % 2) + n, :],
                    in_=r_raw[i][:, 2 * P * n : 2 * P * n + 2 * P].rearrange("p (a k) -> p k a", a=2),
                )

        minus_half = const.tile([P, 2 * HEADS], F32, name="minus_half")
        nc.vector.memset(minus_half[:], -0.5)
        var_eps = stat.tile([P, 2 * HEADS], F32, name="var_eps")

        def last_root():
            nc.vector.tensor_scalar(
                out=var_eps[:],
                in0=moments[3][:].rearrange("p n (a k) -> p (n a) k", a=2)[:, :, 2],
                scalar1=1.0 / P,
                scalar2=EPS,
                op0=ALU.mult,
                op1=ALU.add,
            )
            nc.gpsimd.tensor_tensor(out=rstd[3][:], in0=var_eps[:], in1=minus_half[:], op=ALU.pow)

        def root(j):
            nc.scalar.activation(
                out=rstd[j][:],
                in_=moments[j][:].rearrange("p n (a k) -> p (n a) k", a=2)[:, :, 2],
                func=ACT.Abs_reciprocal_sqrt,
                scale=1.0 / P,
                bias=EPS,
            )

        shift = [stat.tile([P, 2 * HEADS], F32, name="shift%d" % j) for j in range(4)]

        def finish(j):
            nc.vector.scalar_tensor_tensor(
                out=shift[j][:],
                in0=moments[j][:].rearrange("p n (a k) -> p (n a) k", a=2)[:, :, 1],
                scalar=-1.0,
                in1=rstd[j][:],
                op0=ALU.mult,
                op1=ALU.mult,
            )

        cat = {}

        def normalise(i):
            cat[i] = cat_pool.tile([P, 1024], F32, name="cat")
            for c in range(HEADS):
                col = HEADS * (i % 2) + c
                nc.scalar.activation(
                    out=cat[i][:, P * c : P * c + P],
                    in_=r_raw[i][:, P * c : P * c + P],
                    func=ACT.Identity,
                    bias=shift[i // 2][:, col : col + 1],
                    scale=rstd[i // 2][:, col : col + 1],
                )

        def normalise_on_vector(i):
            cat[i] = cat_pool.tile([P, 1024], F32, name="cat")
            for c in range(HEADS):
                col = HEADS * (i % 2) + c
                nc.vector.tensor_scalar(
                    out=cat[i][:, P * c : P * c + P],
                    in0=r_raw[i][:, P * c : P * c + P],
                    scalar1=rstd[i // 2][:, col : col + 1],
                    scalar2=shift[i // 2][:, col : col + 1],
                    op0=ALU.mult,
                    op1=ALU.add,
                )

        x_bank = {}
        x_grouped = {}

        def x_transpose(i):
            words = x_raw[i // 2][:, i % 2, :].bitcast(F32)
            x_bank[i] = bank()
            for gu in range(4):
                nc.tensor.transpose(x_bank[i][:, P * gu : P * gu + P], words[:, P * gu : P * gu + P], identity[:])

        def x_copy(i):
            b, place = i // 4, i % 4
            for g in range(2):
                if place == 0:
                    x_grouped[(g, b)] = grouped_tile("x_or_h", 4)
                nc.scalar.copy(
                    out=x_grouped[(g, b)][:].bitcast(F32)[:, 256 * place : 256 * place + 256].rearrange(
                        "p (r u) -> p r u", u=2
                    ),
                    in_=x_bank[i][:, 256 * g : 256 * g + 256].rearrange("p (u r) -> p r u", u=2),
                )

        def x_quantise(b, g):
            quantise(x_mx[(g, b)], x_grouped[(g, b)])

        w_grouped = {}

        def regroup(copy, w, g, h):
            w_grouped[(w, g, h)] = grouped_tile("w%d%d" % (g, h), 1)
            copy(
                out=w_grouped[(w, g, h)][:].rearrange("p (c i t) -> p c t i", i=4, t=4),
                in_=w_raw[(w, g, h)][:].rearrange("p t (c i) -> p c t i", i=4),
            )

        def regroup_by_tensor(w, g, h):
            w_grouped[(w, g, h)] = grouped_tile("w%d%d" % (g, h), 1)
            for q in range(2):
                words = bank(BF16)
                for u in range(2):
                    nc.tensor.matmul(
                        words[:].rearrange("p (n u e) -> p u n e", u=2, e=2)[:, u],
                        lhsT=identity16[:],
                        rhs=w_raw[(w, g, h)][:, 2 * u : 2 * u + 2, 256 * q : 256 * q + 256].rearrange("p e n -> p n e"),
                        start=True,
                        stop=True,
                    )
                nc.scalar.copy(out=w_grouped[(w, g, h)][:, 1024 * q : 1024 * q + 1024], in_=words[:])

        def w_quantise(w, g, h):
            quantise(w_mx[(w, g, h)], w_grouped[(w, g, h)])

        on_scalar = nc.scalar.copy
        on_vector = nc.vector.tensor_copy

        gate_bank = {}
        gate = {}

        def gate_matmuls(b, c):
            gate_bank[(b, c)] = bank()
            mx_group(
                gate_bank[(b, c)],
                [w_mx[("wg", g, c // 4)] for g in range(2)],
                slice(P * (c % 4), P * (c % 4) + P),
                [x_mx[(g, b)] for g in range(2)],
            )

        def gate_silu(b, c):
            if c % 4 == 0:
                gate[(b, c // 4)] = gate_pool.tile([P, 4, 512], F32, name="gate%d%d" % (b, c // 4))
            nc.scalar.activation(
                out=gate[(b, c // 4)][:, c % 4, :],
                in_=gate_bank[(b, c)][:],
                func=ACT.Silu,
                bias=bg_col[:, c : c + 1],
                scale=1.0,
            )

        cat_bank = {}
        h_grouped = {}

        def cat_transpose(i, g):
            cat_bank[(i, g)] = bank()
            for t in range(4):
                c = 4 * g + t
                nc.tensor.transpose(cat_bank[(i, g)][:, P * t : P * t + P], cat[i][:, P * c : P * c + P], identity[:])

        def multiply(i, g):
            b, place = i // 4, i % 4
            if (g, b) not in h_grouped:
                h_grouped[(g, b)] = grouped_tile("x_or_h", 4)
            nc.vector.tensor_tensor(
                out=h_grouped[(g, b)][:, 512 * place : 512 * place + 512].rearrange("p (c i t) -> p c t i", i=4, t=4),
                in0=gate[(b, g)][:, :, P * place : P * place + P].rearrange("p t (c i) -> p c t i", i=4),
                in1=cat_bank[(i, g)][:].rearrange("p (t c i) -> p c t i", t=4, i=4),
                op=ALU.mult,
            )

        def h_quantise(b, half, g):
            quantise(h_mx[(g, b)], h_grouped[(g, b)], 256 * half, 256)

        out_bank = {}

        def out_matmuls(i, h):
            out_bank[(i, h)] = bank()
            place = i % 4
            mx_group(
                out_bank[(i, h)],
                [h_mx[(g, i // 4)] for g in range(2)],
                slice(P * place, P * place + P),
                [w_mx[("wo", g, h)] for g in range(2)],
            )

        def out_bias(i, h):
            result = out_pool.tile([P, 512], F32, name="result")
            cols = slice(512 * h, 512 * h + 512)
            nc.vector.tensor_tensor(out=result[:], in0=out_bank[(i, h)][:], in1=bo_all[:, cols], op=ALU.add)
            nc.sync.dma_start(out=out_tiles[:, i, cols], in_=result[:])

        load_bg()
        load_table(ACT.Abs_reciprocal_sqrt)
        load_r(0)
        load_r(1)
        load_w("wg", 0, 0)
        load_r(2)
        load_r(3)
        load_x(0)
        load_w("wg", 1, 0)
        load_r(4)
        load_x(1)
        load_w("wg", 0, 1)
        load_r(5)
        load_w("wg", 1, 1)
        load_r(6)
        load_r(7)
        load_x(2)
        load_w("wo", 0, 0)
        load_x(3)
        load_w("wo", 1, 0)
        load_w("wo", 0, 1)
        load_w("wo", 1, 1)
        load_bo()
        statistics(0)
        statistics(1)
        root(0)
        statistics(2)
        finish(0)
        normalise(0)
        regroup_by_tensor("wg", 0, 0)
        x_transpose(0)
        x_transpose(1)
        x_copy(0)
        x_copy(1)
        regroup_by_tensor("wg", 1, 0)
        x_transpose(2)
        x_transpose(3)
        statistics(3)
        normalise_on_vector(1)
        w_quantise("wg", 0, 0)
        root(1)
        x_copy(2)
        x_copy(3)
        bg_columns()
        regroup_by_tensor("wg", 0, 1)
        statistics(4)
        w_quantise("wg", 1, 0)
        finish(1)
        for g in range(2):
            x_quantise(0, g)
        for c in range(4):
            gate_matmuls(0, c)
        statistics(5)
        normalise(2)
        root(2)
        load_table(ACT.Silu)
        w_quantise("wg", 0, 1)
        regroup(on_vector, "wg", 1, 1)
        w_quantise("wg", 1, 1)
        statistics(6)
        for c in range(4, 8):
            gate_matmuls(0, c)
        statistics(7)
        for c in range(8):
            gate_silu(0, c)
        finish(2)
        last_root()
        normalise_on_vector(3)
        for g in range(2):
            for i in range(4):
                cat_transpose(i, g)
        for g in range(2):
            for i in range(4):
                multiply(i, g)
        for i in range(4, 8):
            x_transpose(i)
        normalise(4)
        for i in range(4, 8):
            x_copy(i)
        finish(3)
        for g in range(2):
            x_quantise(1, g)
        normalise(5)
        for c in range(4):
            gate_matmuls(1, c)
        regroup(on_vector, "wo", 0, 0)
        for c in range(4):
            gate_silu(1, c)
        normalise_on_vector(7)
        normalise(6)
        regroup(on_vector, "wo", 1, 0)
        for i in range(4, 8):
            cat_transpose(i, 0)
        for g in range(2):
            w_quantise("wo", g, 0)
        for c in range(4, 8):
            gate_matmuls(1, c)
        for g in range(2):
            for half in range(2):
                h_quantise(0, half, g)
        for c in range(4, 8):
            gate_silu(1, c)
        for i in range(4, 8):
            multiply(i, 0)
        for i in range(4, 8):
            cat_transpose(i, 1)
        regroup(on_scalar, "wo", 0, 1)
        for half in range(2):
            h_quantise(1, half, 0)
        regroup(on_scalar, "wo", 1, 1)
        for i in range(4, 8):
            multiply(i, 1)
        for i in range(4):
            out_matmuls(i, 0)
        w_quantise("wo", 0, 1)
        for half in range(2):
            h_quantise(1, half, 1)
        for i in range(4):
            out_bias(i, 0)
        w_quantise("wo", 1, 1)
        for i in range(4, 8):
            out_matmuls(i, 0)
        for i in range(4):
            out_matmuls(i, 1)
        for i in range(4, 8):
            out_bias(i, 0)
        for i in range(4, 8):
            out_matmuls(i, 1)
        for i in range(8):
            out_bias(i, 1)
